import numpy as np
import ml_dtypes


def mxq(x, axis, fmt="e4m3"):
    dtype, down = {"e4m3": (ml_dtypes.float8_e4m3fn, 7), "e5m2": (ml_dtypes.float8_e5m2, 14)}[fmt]
    v = np.moveaxis(np.asarray(x, np.float32).astype(ml_dtypes.bfloat16).astype(np.float64), axis, -1)
    blocks = v.reshape(v.shape[:-1] + (-1, 32))
    amax = np.abs(blocks).max(-1, keepdims=True)
    byte = np.maximum(np.where(amax > 0, np.frexp(amax)[1] - 1 + 127, 0) - down, 1)
    scale = np.exp2(byte - 127.0)
    codes = (blocks / scale).astype(np.float32).astype(dtype).astype(np.float64)
    return np.moveaxis((codes * scale).reshape(v.shape), -1, axis)


WIDE = False


def mx_kscale(k):
    if not WIDE:
        return np.ones(k)
    levels = np.array([10, -10, 5, -5, 0])
    a = np.random.permutation(np.resize(levels, k // 512 * 4)).reshape(k // 512, 4)
    idx = np.arange(k)
    return np.exp2(a[idx // 512, idx % 128 // 32])


BF16 = ml_dtypes.bfloat16


def bf(x):
    return np.asarray(x, np.float32).astype(BF16)


def f64(x):
    return np.asarray(x).astype(np.float64)


E2M1 = np.array([0.0, 0.5, 1.0, 1.5, 2.0, 3.0, 4.0, 6.0, -0.0, -0.5, -1.0, -1.5, -2.0, -3.0, -4.0, -6.0])


def pack_weight(w, fmt):
    k, n = w.shape
    w = f64(bf(w)).reshape(k // 32, 32, n)
    amax = np.abs(w).max(1)
    if fmt == "e4m3":
        byte = np.frexp(amax)[1] - 1 + 127 - 7
    else:
        mant, ex = np.frexp(amax / 6.0)
        byte = np.where(mant > 0.5, ex, ex - 1) + 127
    byte = np.clip(np.where(amax > 0, byte, 1), 1, 254)
    scaled = (w * np.exp2(127.0 - byte)[:, None, :]).reshape(k, n).astype(np.float32)
    by_word = np.ascontiguousarray(scaled.reshape(k // 512, 128, 4, n).transpose(0, 1, 3, 2))
    if fmt == "e4m3":
        words = by_word.astype(ml_dtypes.float8_e4m3fn).view(np.uint8)
    else:
        c = by_word.astype(ml_dtypes.float4_e2m1fn).view(np.uint8) & 0xF
        words = c[..., 0::2] | (c[..., 1::2] << 4)
    return np.ascontiguousarray(words), np.ascontiguousarray(byte.astype(np.uint8).reshape(k // 512, 16, n))


def unpack_weight(words, scales, fmt):
    g, p, n, _ = words.shape
    if fmt == "e4m3":
        vals = np.ascontiguousarray(words).view(ml_dtypes.float8_e4m3fn).astype(np.float64)
    else:
        nib = np.empty((g, p, n, 4), np.uint8)
        nib[..., 0::2] = words & 0xF
        nib[..., 1::2] = words >> 4
        vals = E2M1[nib]
    vals = vals * np.repeat(np.exp2(scales.astype(np.float64) - 127.0), 8, axis=1)[..., None]
    return vals.transpose(0, 1, 3, 2).reshape(g * 512, n)


B, I, U = 512, 1024, 1024


def sigmoid(v):
    return 1.0 / (1.0 + np.exp(-v))


def setup_inputs():
    s = mx_kscale(I)
    x_t = bf(np.random.standard_normal((B, I)) * s)
    h_tm1 = bf(np.random.standard_normal((B, U)))
    iw_words, iw_scales = pack_weight(np.random.standard_normal((I, U * 3)) / np.sqrt(I) / s[:, None], "e4m3")
    hw_words, hw_scales = pack_weight(np.random.standard_normal((U, U * 3)) / np.sqrt(U), "e4m3")
    bias = bf(np.random.standard_normal(U * 3) * 0.1)
    return {"x_t": x_t,
            "h_tm1": h_tm1,
            "input_weight_words": iw_words,
            "input_weight_scales": iw_scales,
            "hidden_state_weight_words": hw_words,
            "hidden_state_weight_scales": hw_scales,
            "bias": bias}


def reference(x_t, h_tm1, input_weight_words, input_weight_scales, hidden_state_weight_words, hidden_state_weight_scales, bias):
    u = U
    x, h, b = f64(x_t), f64(h_tm1), f64(bias)
    whq = unpack_weight(hidden_state_weight_words, hidden_state_weight_scales, "e4m3")
    xg = mxq(x, 1, "e4m3") @ unpack_weight(input_weight_words, input_weight_scales, "e4m3")
    xr, xu, xh = xg[:, :u], xg[:, u:2 * u], xg[:, 2 * u:]
    hg = mxq(h, 1, "e4m3") @ whq[:, :2 * u]
    hr, hu = hg[:, :u], hg[:, u:]
    br, bu_, bh = b[:u], b[u:2 * u], b[2 * u:]
    r_t = sigmoid(xr + hr + br)
    u_t = sigmoid(xu + hu + bu_)
    cand = np.tanh(xh + (mxq(r_t * h, 1, "e4m3") @ whq[:, 2 * u:]) + bh)
    h_t = u_t * h + (1.0 - u_t) * cand
    return h_t

@@ -1,0 +1,239 @@
+from contextlib import ExitStack
+
+import concourse.mybir as mybir
+from concourse.masks import make_identity
+
+F32 = mybir.dt.float32
+BF16 = mybir.dt.bfloat16
+I32 = mybir.dt.int32
+U32 = mybir.dt.uint32
+U8 = mybir.dt.uint8
+FP8X4 = mybir.dt.float8_e4m3fn_x4
+ALU = mybir.AluOpType
+ACT = mybir.ActivationFunctionType
+
+P = 128
+PACK = 4
+K_PASS = P * PACK
+BATCH = 512
+WIDTH = 1024
+BT = BATCH // P
+G = WIDTH // K_PASS
+KC = 2 * G
+N_TILE = 512
+NH = WIDTH // N_TILE
+RESET, UPDATE, CAND = 0, 1, 2
+
+FLOPS = 2 * BATCH * WIDTH * (3 * WIDTH + 2 * WIDTH + WIDTH)
+
+
+def by_word_slot(ap):
+    return ap.rearrange("b (p t) -> b t p", t=PACK)
+
+
+def tile_anothergrucell_kernel(
+    tc, x_t, h_tm1, iw_words, iw_scales, hw_words, hw_scales, bias, out
+):
+    nc = tc.nc
+    with ExitStack() as ctx:
+        keep = ctx.enter_context(tc.tile_pool(name="keep", bufs=1))
+        work = ctx.enter_context(tc.tile_pool(name="work", bufs=4))
+        psum_t = ctx.enter_context(tc.psum_pool(name="psum_t", bufs=4))
+        psum_acc = ctx.enter_context(tc.psum_pool(name="psum_acc", bufs=4))
+
+        w_planes = keep.tile([P, 3 * WIDTH], U8, align_bytes=64)
+        nc.vector.memset(w_planes[:].bitcast(I32), 0)
+        bias_row = keep.tile([P, 3 * WIDTH], BF16)
+        nc.vector.memset(bias_row[:].bitcast(I32), 0)
+        ones = keep.tile([P, P], BF16)
+        nc.vector.memset(ones[:], 1.0)
+        ident = keep.tile([P, P], F32)
+        make_identity(nc, ident[:])
+
+        act_sb = keep.tile([P, 2, BT, WIDTH], BF16)
+        for bt in range(BT):
+            rows = slice(bt * P, (bt + 1) * P)
+            nc.sync.dma_start(out=act_sb[:, 0, bt, :], in_=x_t[rows, :])
+            nc.sync.dma_start(out=act_sb[:, 1, bt, :], in_=h_tm1[rows, :])
+        nc.scalar.dma_start(out=bias_row[0:1, :], in_=bias.rearrange("(o n) -> o n", o=1))
+
+        for w, scales in enumerate((iw_scales, hw_scales)):
+            for q in range(4):
+                first = 32 * q + 2 * PACK * w
+                nc.sync.dma_start(
+                    out=w_planes[first : first + 2 * PACK, :].bitcast(I32),
+                    in_=scales[:, PACK * q : PACK * (q + 1), :].bitcast(I32),
+                )
+
+        w_words = keep.tile([P, KC, 3 * WIDTH], U32, align_bytes=64)
+
+        def load_weight_columns(first, width):
+            for kc in range(KC):
+                words = (iw_words, hw_words)[kc // G][kc % G]
+                nc.sync.dma_start(
+                    out=w_words[:, kc, first : first + width].bitcast(I32),
+                    in_=words.rearrange("p n t -> p (n t)")[
+                        :, PACK * first : PACK * (first + width)
+                    ].bitcast(I32),
+                )
+
+        load_weight_columns(RESET * WIDTH, N_TILE)
+        load_weight_columns(RESET * WIDTH + N_TILE, N_TILE)
+        load_weight_columns(UPDATE * WIDTH, WIDTH)
+        load_weight_columns(CAND * WIDTH, WIDTH)
+
+        bias_bc = keep.tile([P, 3, WIDTH], F32)
+
+        def broadcast_bias(gate):
+            for nh in range(NH):
+                cols = slice(nh * N_TILE, (nh + 1) * N_TILE)
+                acc = psum_acc.tile([P, N_TILE], F32, tag="acc")
+                nc.tensor.matmul(
+                    out=acc[:],
+                    lhsT=ones[:],
+                    rhs=bias_row[:, gate * WIDTH + nh * N_TILE : gate * WIDTH + (nh + 1) * N_TILE],
+                    start=True,
+                    stop=True,
+                )
+                if gate == RESET:
+                    nc.scalar.copy(
+                        out=bias_bc[:, gate, cols].rearrange("b (t p) -> b t p", t=PACK),
+                        in_=by_word_slot(acc[:]),
+                    )
+                else:
+                    nc.scalar.copy(out=bias_bc[:, gate, cols], in_=acc[:])
+
+        grouped = keep.tile([P, BT, KC, P, PACK], BF16, align_bytes=64)
+        act_codes = keep.tile([P, BT, KC, P], U32, align_bytes=64)
+        act_planes = keep.tile([P, BT, KC, P], U8, align_bytes=64)
+
+        def transpose_and_quantise(bt):
+            for s in range(2):
+                words = act_sb[:, s, bt, :].bitcast(F32)
+                bank = psum_t.tile([P, PACK, P], F32, tag="bank")
+                for g in range(G):
+                    for u in range(2):
+                        nc.tensor.transpose(
+                            out=bank[:, 2 * g + u, :],
+                            in_=words[:, 256 * g + u : 256 * (g + 1) : 2],
+                            identity=ident[:],
+                        )
+                nc.scalar.copy(
+                    out=grouped[:, bt, G * s : G * (s + 1), :, :].bitcast(F32),
+                    in_=bank[:].rearrange("p (g u) b -> p g b u", u=2),
+                )
+            nc.vector.quantize_mx(
+                out=act_codes[:, bt].rearrange("p c b -> p (c b)").bitcast(FP8X4),
+                scales=act_planes[:, bt].rearrange("p c b -> p (c b)"),
+                in_=grouped[:, bt].rearrange("p c b t -> p (c b t)"),
+            )
+
+        rh_grouped = keep.tile([P, BT, G, P, PACK], BF16, align_bytes=64)
+        rh_codes = keep.tile([P, BT, G, P], U32, align_bytes=64)
+        rh_planes = keep.tile([P, BT, G, P], U8, align_bytes=64)
+
+        def gate_sums(bt, gate, nh):
+            first = gate * WIDTH + nh * N_TILE
+            acc = psum_acc.tile([P, N_TILE], F32, tag="acc")
+            for kc in range(KC):
+                if gate == CAND and kc >= G:
+                    codes, planes = rh_codes[:, bt, kc - G, :], rh_planes[:, bt, kc - G, :]
+                else:
+                    codes, planes = act_codes[:, bt, kc, :], act_planes[:, bt, kc, :]
+                nc.tensor.matmul_mx(
+                    out=acc[:],
+                    lhsT=codes.bitcast(FP8X4),
+                    lhsT_scale=planes,
+                    rhs=w_words[:, kc, first : first + N_TILE].bitcast(FP8X4),
+                    rhs_scale=w_planes[PACK * kc : P, first : first + N_TILE],
+                    start=(kc == 0),
+                    stop=(kc == KC - 1),
+                )
+            return acc
+
+        r_all = keep.tile([P, BT, G, PACK, P], F32)
+
+        def reset_gate(g, bt):
+            acc = gate_sums(bt, RESET, g)
+            nc.vector.tensor_tensor(
+                out=r_all[:, bt, g],
+                in0=by_word_slot(acc[:]),
+                in1=bias_bc[:, RESET, g * N_TILE : (g + 1) * N_TILE].rearrange(
+                    "b (t p) -> b t p", t=PACK
+                ),
+                op=ALU.add,
+            )
+            nc.scalar.activation(out=r_all[:, bt, g], in_=r_all[:, bt, g], func=ACT.Sigmoid)
+
+        def reset_times_h(g, bt):
+            bank = psum_t.tile([P, PACK, P], F32, tag="bank")
+            for t in range(PACK):
+                nc.tensor.transpose(out=bank[:, t, :], in_=r_all[:, bt, g, t, :], identity=ident[:])
+            nc.vector.tensor_tensor(
+                out=rh_grouped[:, bt, g],
+                in0=bank[:].rearrange("p t b -> p b t"),
+                in1=grouped[:, bt, G + g],
+                op=ALU.mult,
+            )
+
+        def quantise_rh(bt):
+            nc.vector.quantize_mx(
+                out=rh_codes[:, bt].rearrange("p g b -> p (g b)").bitcast(FP8X4),
+                scales=rh_planes[:, bt].rearrange("p g b -> p (g b)"),
+                in_=rh_grouped[:, bt].rearrange("p g b t -> p (g b t)"),
+            )
+
+        u_all = keep.tile([P, BT, WIDTH], F32)
+        uh_all = keep.tile([P, BT, WIDTH], F32)
+
+        def update_gate(bt):
+            for nh in range(NH):
+                cols = slice(nh * N_TILE, (nh + 1) * N_TILE)
+                acc = gate_sums(bt, UPDATE, nh)
+                nc.vector.tensor_tensor(
+                    out=u_all[:, bt, cols], in0=acc[:], in1=bias_bc[:, UPDATE, cols], op=ALU.add
+                )
+                nc.scalar.activation(out=u_all[:, bt, cols], in_=u_all[:, bt, cols], func=ACT.Sigmoid)
+                nc.gpsimd.tensor_tensor(
+                    out=uh_all[:, bt, cols], in0=u_all[:, bt, cols], in1=act_sb[:, 1, bt, cols], op=ALU.mult
+                )
+
+        def candidate_and_blend(bt):
+            for nh in range(NH):
+                cols = slice(nh * N_TILE, (nh + 1) * N_TILE)
+                acc = gate_sums(bt, CAND, nh)
+                cand = work.tile([P, N_TILE], F32, tag="cand")
+                nc.vector.tensor_tensor(out=cand[:], in0=acc[:], in1=bias_bc[:, CAND, cols], op=ALU.add)
+                nc.scalar.activation(out=cand[:], in_=cand[:], func=ACT.Tanh)
+                part = work.tile([P, N_TILE], F32, tag="part")
+                nc.vector.scalar_tensor_tensor(
+                    out=part[:], in0=u_all[:, bt, cols], scalar=1.0, in1=cand[:],
+                    op0=ALU.subtract, op1=ALU.mult,
+                )
+                h_new = work.tile([P, N_TILE], F32, tag="h_new")
+                nc.vector.tensor_tensor(out=h_new[:], in0=uh_all[:, bt, cols], in1=part[:], op=ALU.subtract)
+                nc.sync.dma_start(out=out[bt * P : (bt + 1) * P, cols], in_=h_new[:])
+
+        for bt in range(BT):
+            transpose_and_quantise(bt)
+        for gate in range(3):
+            broadcast_bias(gate)
+        for bt in range(BT):
+            reset_gate(0, bt)
+        reset_gate(1, 0)
+        reset_gate(1, 1)
+        for bt in range(BT):
+            reset_times_h(0, bt)
+        reset_gate(1, 2)
+        reset_gate(1, 3)
+        update_gate(0)
+        for bt in range(BT):
+            reset_times_h(1, bt)
+            quantise_rh(bt)
+        update_gate(1)
+        candidate_and_blend(0)
+        update_gate(2)
+        candidate_and_blend(1)
+        update_gate(3)
+        candidate_and_blend(2)
+        candidate_and_blend(3)

@@ -23,11 +23,12 @@ KC = 2 * G
 N_TILE = 512
 NH = WIDTH // N_TILE
 RESET, UPDATE, CAND = 0, 1, 2
+X, H = 0, 1
 
 FLOPS = 2 * BATCH * WIDTH * (3 * WIDTH + 2 * WIDTH + WIDTH)
 
 
-def by_word_slot(ap):
+def by_byte_then_partition(ap):
     return ap.rearrange("b (p t) -> b t p", t=PACK)
 
 
@@ -36,10 +37,11 @@ def tile_anothergrucell_kernel(
 ):
     nc = tc.nc
     with ExitStack() as ctx:
+        ctx.enter_context(tc.manual_schedule())
         keep = ctx.enter_context(tc.tile_pool(name="keep", bufs=1))
         work = ctx.enter_context(tc.tile_pool(name="work", bufs=4))
-        psum_t = ctx.enter_context(tc.psum_pool(name="psum_t", bufs=4))
-        psum_acc = ctx.enter_context(tc.psum_pool(name="psum_acc", bufs=4))
+        psum_t = ctx.enter_context(tc.psum_pool(name="psum_t", bufs=3))
+        psum_acc = ctx.enter_context(tc.psum_pool(name="psum_acc", bufs=5))
 
         w_planes = keep.tile([P, 3 * WIDTH], U8, align_bytes=64)
         nc.vector.memset(w_planes[:].bitcast(I32), 0)
@@ -49,19 +51,22 @@ def tile_anothergrucell_kernel(
         nc.vector.memset(ones[:], 1.0)
         ident = keep.tile([P, P], F32)
         make_identity(nc, ident[:])
+        warm = keep.tile([P, 1], F32)
+        nc.scalar.activation(out=warm[:], in_=ones[:, 0:1], func=ACT.Sigmoid)
 
-        act_sb = keep.tile([P, 2, BT, WIDTH], BF16)
+        act_sb = [[None] * BT, [None] * BT]
         for bt in range(BT):
             rows = slice(bt * P, (bt + 1) * P)
-            nc.sync.dma_start(out=act_sb[:, 0, bt, :], in_=x_t[rows, :])
-            nc.sync.dma_start(out=act_sb[:, 1, bt, :], in_=h_tm1[rows, :])
+            for s, source in enumerate((x_t, h_tm1)):
+                act_sb[s][bt] = keep.tile([P, WIDTH], BF16, name="act_sb_%d_%d" % (s, bt))
+                nc.sync.dma_start(out=act_sb[s][bt][:], in_=source[rows, :])
         nc.scalar.dma_start(out=bias_row[0:1, :], in_=bias.rearrange("(o n) -> o n", o=1))
 
         for w, scales in enumerate((iw_scales, hw_scales)):
             for q in range(4):
-                first = 32 * q + 2 * PACK * w
+                first = 32 * q + G * PACK * w
                 nc.sync.dma_start(
-                    out=w_planes[first : first + 2 * PACK, :].bitcast(I32),
+                    out=w_planes[first : first + G * PACK, :].bitcast(I32),
                     in_=scales[:, PACK * q : PACK * (q + 1), :].bitcast(I32),
                 )
 
@@ -82,58 +87,57 @@ def tile_anothergrucell_kernel(
         load_weight_columns(UPDATE * WIDTH, WIDTH)
         load_weight_columns(CAND * WIDTH, WIDTH)
 
-        bias_bc = keep.tile([P, 3, WIDTH], F32)
-
-        def broadcast_bias(gate):
-            for nh in range(NH):
-                cols = slice(nh * N_TILE, (nh + 1) * N_TILE)
-                acc = psum_acc.tile([P, N_TILE], F32, tag="acc")
-                nc.tensor.matmul(
-                    out=acc[:],
-                    lhsT=ones[:],
-                    rhs=bias_row[:, gate * WIDTH + nh * N_TILE : gate * WIDTH + (nh + 1) * N_TILE],
-                    start=True,
-                    stop=True,
-                )
-                if gate == RESET:
-                    nc.scalar.copy(
-                        out=bias_bc[:, gate, cols].rearrange("b (t p) -> b t p", t=PACK),
-                        in_=by_word_slot(acc[:]),
-                    )
-                else:
-                    nc.scalar.copy(out=bias_bc[:, gate, cols], in_=acc[:])
-
         grouped = keep.tile([P, BT, KC, P, PACK], BF16, align_bytes=64)
         act_codes = keep.tile([P, BT, KC, P], U32, align_bytes=64)
         act_planes = keep.tile([P, BT, KC, P], U8, align_bytes=64)
 
-        def transpose_and_quantise(bt):
-            for s in range(2):
-                words = act_sb[:, s, bt, :].bitcast(F32)
+        def transpose_inputs(bt):
+            for s in (X, H):
+                words = act_sb[s][bt][:].bitcast(F32)
                 bank = psum_t.tile([P, PACK, P], F32, tag="bank")
                 for g in range(G):
-                    for u in range(2):
+                    for half in range(2):
                         nc.tensor.transpose(
-                            out=bank[:, 2 * g + u, :],
-                            in_=words[:, 256 * g + u : 256 * (g + 1) : 2],
+                            out=bank[:, 2 * g + half, :],
+                            in_=words[:, g * K_PASS // 2 + half : (g + 1) * K_PASS // 2 : 2],
                             identity=ident[:],
                         )
                 nc.scalar.copy(
                     out=grouped[:, bt, G * s : G * (s + 1), :, :].bitcast(F32),
-                    in_=bank[:].rearrange("p (g u) b -> p g b u", u=2),
+                    in_=bank[:].rearrange("p (g half) b -> p g b half", half=2),
                 )
+
+        def quantise_inputs(bt):
             nc.vector.quantize_mx(
                 out=act_codes[:, bt].rearrange("p c b -> p (c b)").bitcast(FP8X4),
                 scales=act_planes[:, bt].rearrange("p c b -> p (c b)"),
                 in_=grouped[:, bt].rearrange("p c b t -> p (c b t)"),
             )
 
+        bias_bc = keep.tile([P, 3, WIDTH], F32)
+
+        def broadcast_bias(gate):
+            for nh in range(NH):
+                cols = slice(nh * N_TILE, (nh + 1) * N_TILE)
+                first = gate * WIDTH + nh * N_TILE
+                acc = psum_acc.tile([P, N_TILE], F32, tag="acc")
+                nc.tensor.matmul(
+                    out=acc[:], lhsT=ones[:], rhs=bias_row[:, first : first + N_TILE], start=True, stop=True
+                )
+                if gate == RESET:
+                    nc.vector.tensor_copy(
+                        out=bias_bc[:, gate, cols].rearrange("b (t p) -> b t p", t=PACK),
+                        in_=by_byte_then_partition(acc[:]),
+                    )
+                else:
+                    nc.vector.tensor_copy(out=bias_bc[:, gate, cols], in_=acc[:])
+
         rh_grouped = keep.tile([P, BT, G, P, PACK], BF16, align_bytes=64)
         rh_codes = keep.tile([P, BT, G, P], U32, align_bytes=64)
         rh_planes = keep.tile([P, BT, G, P], U8, align_bytes=64)
 
-        def gate_sums(bt, gate, nh):
-            first = gate * WIDTH + nh * N_TILE
+        def gate_sums(bt, gate, start, width):
+            first = gate * WIDTH + start
             acc = psum_acc.tile([P, N_TILE], F32, tag="acc")
             for kc in range(KC):
                 if gate == CAND and kc >= G:
@@ -141,26 +145,24 @@ def tile_anothergrucell_kernel(
                 else:
                     codes, planes = act_codes[:, bt, kc, :], act_planes[:, bt, kc, :]
                 nc.tensor.matmul_mx(
-                    out=acc[:],
+                    out=acc[:, :width],
                     lhsT=codes.bitcast(FP8X4),
                     lhsT_scale=planes,
-                    rhs=w_words[:, kc, first : first + N_TILE].bitcast(FP8X4),
-                    rhs_scale=w_planes[PACK * kc : P, first : first + N_TILE],
+                    rhs=w_words[:, kc, first : first + width].bitcast(FP8X4),
+                    rhs_scale=w_planes[PACK * kc : P, first : first + width],
                     start=(kc == 0),
                     stop=(kc == KC - 1),
                 )
-            return acc
+            return acc[:, :width]
 
         r_all = keep.tile([P, BT, G, PACK, P], F32)
 
         def reset_gate(g, bt):
-            acc = gate_sums(bt, RESET, g)
+            acc = gate_sums(bt, RESET, g * N_TILE, N_TILE)
             nc.vector.tensor_tensor(
                 out=r_all[:, bt, g],
-                in0=by_word_slot(acc[:]),
-                in1=bias_bc[:, RESET, g * N_TILE : (g + 1) * N_TILE].rearrange(
-                    "b (t p) -> b t p", t=PACK
-                ),
+                in0=by_byte_then_partition(acc),
+                in1=bias_bc[:, RESET, g * N_TILE : (g + 1) * N_TILE].rearrange("b (t p) -> b t p", t=PACK),
                 op=ALU.add,
             )
             nc.scalar.activation(out=r_all[:, bt, g], in_=r_all[:, bt, g], func=ACT.Sigmoid)
@@ -172,7 +174,7 @@ def tile_anothergrucell_kernel(
             nc.vector.tensor_tensor(
                 out=rh_grouped[:, bt, g],
                 in0=bank[:].rearrange("p t b -> p b t"),
-                in1=grouped[:, bt, G + g],
+                in1=grouped[:, bt, G * H + g],
                 op=ALU.mult,
             )
 
@@ -186,38 +188,44 @@ def tile_anothergrucell_kernel(
         u_all = keep.tile([P, BT, WIDTH], F32)
         uh_all = keep.tile([P, BT, WIDTH], F32)
 
-        def update_gate(bt):
-            for nh in range(NH):
-                cols = slice(nh * N_TILE, (nh + 1) * N_TILE)
-                acc = gate_sums(bt, UPDATE, nh)
-                nc.vector.tensor_tensor(
-                    out=u_all[:, bt, cols], in0=acc[:], in1=bias_bc[:, UPDATE, cols], op=ALU.add
-                )
-                nc.scalar.activation(out=u_all[:, bt, cols], in_=u_all[:, bt, cols], func=ACT.Sigmoid)
-                nc.gpsimd.tensor_tensor(
-                    out=uh_all[:, bt, cols], in0=u_all[:, bt, cols], in1=act_sb[:, 1, bt, cols], op=ALU.mult
-                )
+        def update_gate(bt, nh):
+            cols = slice(nh * N_TILE, (nh + 1) * N_TILE)
+            acc = gate_sums(bt, UPDATE, nh * N_TILE, N_TILE)
+            nc.vector.tensor_tensor(out=u_all[:, bt, cols], in0=acc, in1=bias_bc[:, UPDATE, cols], op=ALU.add)
+            nc.scalar.activation(out=u_all[:, bt, cols], in_=u_all[:, bt, cols], func=ACT.Sigmoid)
+            nc.gpsimd.tensor_tensor(
+                out=uh_all[:, bt, cols], in0=u_all[:, bt, cols], in1=act_sb[H][bt][:, cols], op=ALU.mult
+            )
 
-        def candidate_and_blend(bt):
-            for nh in range(NH):
-                cols = slice(nh * N_TILE, (nh + 1) * N_TILE)
-                acc = gate_sums(bt, CAND, nh)
-                cand = work.tile([P, N_TILE], F32, tag="cand")
-                nc.vector.tensor_tensor(out=cand[:], in0=acc[:], in1=bias_bc[:, CAND, cols], op=ALU.add)
-                nc.scalar.activation(out=cand[:], in_=cand[:], func=ACT.Tanh)
-                part = work.tile([P, N_TILE], F32, tag="part")
-                nc.vector.scalar_tensor_tensor(
-                    out=part[:], in0=u_all[:, bt, cols], scalar=1.0, in1=cand[:],
-                    op0=ALU.subtract, op1=ALU.mult,
-                )
-                h_new = work.tile([P, N_TILE], F32, tag="h_new")
-                nc.vector.tensor_tensor(out=h_new[:], in0=uh_all[:, bt, cols], in1=part[:], op=ALU.subtract)
-                nc.sync.dma_start(out=out[bt * P : (bt + 1) * P, cols], in_=h_new[:])
+        def candidate(bt, start, width):
+            cols = slice(start, start + width)
+            acc = gate_sums(bt, CAND, start, width)
+            cand = work.tile([P, N_TILE], F32, tag="cand")
+            nc.vector.tensor_tensor(out=cand[:, :width], in0=acc, in1=bias_bc[:, CAND, cols], op=ALU.add)
+            nc.scalar.activation(out=cand[:, :width], in_=cand[:, :width], func=ACT.Tanh)
+            return cand[:, :width]
 
-        for bt in range(BT):
-            transpose_and_quantise(bt)
-        for gate in range(3):
-            broadcast_bias(gate)
+        def blend(bt, start, width, cand, subtract_engine):
+            cols = slice(start, start + width)
+            rest = work.tile([P, N_TILE], F32, tag="rest")
+            nc.vector.scalar_tensor_tensor(
+                out=rest[:, :width], in0=u_all[:, bt, cols], scalar=1.0, in1=cand, op0=ALU.subtract, op1=ALU.mult
+            )
+            h_new = work.tile([P, N_TILE], F32, tag="h_new")
+            subtract_engine.tensor_tensor(
+                out=h_new[:, :width], in0=uh_all[:, bt, cols], in1=rest[:, :width], op=ALU.subtract
+            )
+            nc.sync.dma_start(out=out[bt * P : (bt + 1) * P, cols], in_=h_new[:, :width])
+
+        transpose_inputs(0)
+        for bt in range(1, BT):
+            transpose_inputs(bt)
+            quantise_inputs(bt - 1)
+        broadcast_bias(RESET)
+        quantise_inputs(BT - 1)
+        broadcast_bias(UPDATE)
+        broadcast_bias(CAND)
+
         for bt in range(BT):
             reset_gate(0, bt)
         reset_gate(1, 0)
@@ -226,14 +234,27 @@ def tile_anothergrucell_kernel(
             reset_times_h(0, bt)
         reset_gate(1, 2)
         reset_gate(1, 3)
-        update_gate(0)
+        reset_times_h(1, 0)
+        reset_times_h(1, 1)
+        update_gate(0, 0)
+        quantise_rh(0)
+        quantise_rh(1)
+        reset_times_h(1, 2)
+        reset_times_h(1, 3)
+        update_gate(0, 1)
+        quantise_rh(2)
+        quantise_rh(3)
+
         for bt in range(BT):
-            reset_times_h(1, bt)
-            quantise_rh(bt)
-        update_gate(1)
-        candidate_and_blend(0)
-        update_gate(2)
-        candidate_and_blend(1)
-        update_gate(3)
-        candidate_and_blend(2)
-        candidate_and_blend(3)
+            if bt + 1 < BT:
+                pieces = [(0, N_TILE), (N_TILE, N_TILE)]
+                engines = [nc.vector, nc.gpsimd]
+            else:
+                pieces = [(0, N_TILE), (N_TILE, N_TILE // 2), (N_TILE + N_TILE // 2, N_TILE // 2)]
+                engines = [nc.vector, nc.vector, nc.vector]
+            cands = [candidate(bt, start, width) for start, width in pieces]
+            for (start, width), cand, engine in zip(pieces, cands, engines):
+                blend(bt, start, width, cand, engine)
+            if bt + 1 < BT:
+                for nh in range(NH):
+                    update_gate(bt + 1, nh)

@@ -43,10 +43,11 @@ def tile_anothergrucell_kernel(
         psum_t = ctx.enter_context(tc.psum_pool(name="psum_t", bufs=3))
         psum_acc = ctx.enter_context(tc.psum_pool(name="psum_acc", bufs=5))
 
-        w_planes = keep.tile([P, 3 * WIDTH], U8, align_bytes=64)
-        nc.vector.memset(w_planes[:].bitcast(I32), 0)
         bias_row = keep.tile([P, 3 * WIDTH], BF16)
         nc.vector.memset(bias_row[:].bitcast(I32), 0)
+        nc.scalar.dma_start(out=bias_row[0:1, :], in_=bias.rearrange("(o n) -> o n", o=1))
+        w_planes = keep.tile([P, 3 * WIDTH], U8, align_bytes=64)
+        nc.vector.memset(w_planes[:].bitcast(I32), 0)
         ones = keep.tile([P, P], BF16)
         nc.vector.memset(ones[:], 1.0)
         ident = keep.tile([P, P], F32)
@@ -54,36 +55,38 @@ def tile_anothergrucell_kernel(
         warm = keep.tile([P, 1], F32)
         nc.scalar.activation(out=warm[:], in_=ones[:, 0:1], func=ACT.Sigmoid)
 
-        act_sb = [[None] * BT, [None] * BT]
-        for bt in range(BT):
-            rows = slice(bt * P, (bt + 1) * P)
+        act_sb = [keep.tile([P, BT, WIDTH], BF16, name="x_sb"), keep.tile([P, BT, WIDTH], BF16, name="h_sb")]
+        for first_bt in range(0, BT, 2):
             for s, source in enumerate((x_t, h_tm1)):
-                act_sb[s][bt] = keep.tile([P, WIDTH], BF16, name="act_sb_%d_%d" % (s, bt))
-                nc.sync.dma_start(out=act_sb[s][bt][:], in_=source[rows, :])
-        nc.scalar.dma_start(out=bias_row[0:1, :], in_=bias.rearrange("(o n) -> o n", o=1))
-
-        for w, scales in enumerate((iw_scales, hw_scales)):
-            for q in range(4):
-                first = 32 * q + G * PACK * w
                 nc.sync.dma_start(
-                    out=w_planes[first : first + G * PACK, :].bitcast(I32),
-                    in_=scales[:, PACK * q : PACK * (q + 1), :].bitcast(I32),
+                    out=act_sb[s][:, first_bt : first_bt + 2, :],
+                    in_=source[first_bt * P : (first_bt + 2) * P, :].rearrange("(t p) k -> p t k", p=P),
                 )
 
         w_words = keep.tile([P, KC, 3 * WIDTH], U32, align_bytes=64)
 
+        def load_scale_columns(first, width):
+            for w, scales in enumerate((iw_scales, hw_scales)):
+                for q in range(4):
+                    row = 32 * q + G * PACK * w
+                    nc.sync.dma_start(
+                        out=w_planes[row : row + G * PACK, first : first + width].bitcast(I32),
+                        in_=scales[:, PACK * q : PACK * (q + 1), first : first + width].bitcast(I32),
+                    )
+
         def load_weight_columns(first, width):
-            for kc in range(KC):
-                words = (iw_words, hw_words)[kc // G][kc % G]
+            for w, words in enumerate((iw_words, hw_words)):
                 nc.sync.dma_start(
-                    out=w_words[:, kc, first : first + width].bitcast(I32),
-                    in_=words.rearrange("p n t -> p (n t)")[
-                        :, PACK * first : PACK * (first + width)
+                    out=w_words[:, G * w : G * (w + 1), first : first + width].bitcast(I32),
+                    in_=words.rearrange("g p n t -> p g (n t)")[
+                        :, :, PACK * first : PACK * (first + width)
                     ].bitcast(I32),
                 )
 
+        load_scale_columns(RESET * WIDTH, WIDTH)
         load_weight_columns(RESET * WIDTH, N_TILE)
         load_weight_columns(RESET * WIDTH + N_TILE, N_TILE)
+        load_scale_columns(UPDATE * WIDTH, 2 * WIDTH)
         load_weight_columns(UPDATE * WIDTH, WIDTH)
         load_weight_columns(CAND * WIDTH, WIDTH)
 
@@ -93,7 +96,7 @@ def tile_anothergrucell_kernel(
 
         def transpose_inputs(bt):
             for s in (X, H):
-                words = act_sb[s][bt][:].bitcast(F32)
+                words = act_sb[s][:, bt, :].bitcast(F32)
                 bank = psum_t.tile([P, PACK, P], F32, tag="bank")
                 for g in range(G):
                     for half in range(2):
@@ -194,7 +197,7 @@ def tile_anothergrucell_kernel(
             nc.vector.tensor_tensor(out=u_all[:, bt, cols], in0=acc, in1=bias_bc[:, UPDATE, cols], op=ALU.add)
             nc.scalar.activation(out=u_all[:, bt, cols], in_=u_all[:, bt, cols], func=ACT.Sigmoid)
             nc.gpsimd.tensor_tensor(
-                out=uh_all[:, bt, cols], in0=u_all[:, bt, cols], in1=act_sb[H][bt][:, cols], op=ALU.mult
+                out=uh_all[:, bt, cols], in0=u_all[:, bt, cols], in1=act_sb[H][:, bt, cols], op=ALU.mult
             )
 
         def candidate(bt, start, width):
@@ -205,16 +208,22 @@ def tile_anothergrucell_kernel(
             nc.scalar.activation(out=cand[:, :width], in_=cand[:, :width], func=ACT.Tanh)
             return cand[:, :width]
 
-        def blend(bt, start, width, cand, subtract_engine):
-            cols = slice(start, start + width)
+        def blend_product(bt, start, width, cand):
             rest = work.tile([P, N_TILE], F32, tag="rest")
             nc.vector.scalar_tensor_tensor(
-                out=rest[:, :width], in0=u_all[:, bt, cols], scalar=1.0, in1=cand, op0=ALU.subtract, op1=ALU.mult
+                out=rest[:, :width],
+                in0=u_all[:, bt, start : start + width],
+                scalar=1.0,
+                in1=cand,
+                op0=ALU.subtract,
+                op1=ALU.mult,
             )
+            return rest[:, :width]
+
+        def blend_and_store(bt, start, width, rest):
+            cols = slice(start, start + width)
             h_new = work.tile([P, N_TILE], F32, tag="h_new")
-            subtract_engine.tensor_tensor(
-                out=h_new[:, :width], in0=uh_all[:, bt, cols], in1=rest[:, :width], op=ALU.subtract
-            )
+            nc.vector.tensor_tensor(out=h_new[:, :width], in0=uh_all[:, bt, cols], in1=rest, op=ALU.subtract)
             nc.sync.dma_start(out=out[bt * P : (bt + 1) * P, cols], in_=h_new[:, :width])
 
         transpose_inputs(0)
@@ -245,16 +254,19 @@ def tile_anothergrucell_kernel(
         quantise_rh(2)
         quantise_rh(3)
 
-        for bt in range(BT):
-            if bt + 1 < BT:
-                pieces = [(0, N_TILE), (N_TILE, N_TILE)]
-                engines = [nc.vector, nc.gpsimd]
-            else:
-                pieces = [(0, N_TILE), (N_TILE, N_TILE // 2), (N_TILE + N_TILE // 2, N_TILE // 2)]
-                engines = [nc.vector, nc.vector, nc.vector]
-            cands = [candidate(bt, start, width) for start, width in pieces]
-            for (start, width), cand, engine in zip(pieces, cands, engines):
-                blend(bt, start, width, cand, engine)
-            if bt + 1 < BT:
-                for nh in range(NH):
-                    update_gate(bt + 1, nh)
+        pieces = [(bt, nh * N_TILE, N_TILE) for bt in range(BT) for nh in range(NH)]
+        pieces[-1:] = [(BT - 1, WIDTH - N_TILE, N_TILE // 2), (BT - 1, WIDTH - N_TILE // 2, N_TILE // 2)]
+        cands = []
+        rests = []
+        for i in range(len(pieces) + 2):
+            if i < len(pieces):
+                bt, start, width = pieces[i]
+                cands.append(candidate(bt, start, width))
+                if bt + 1 < BT:
+                    update_gate(bt + 1, start // N_TILE)
+            if 1 <= i <= len(pieces):
+                bt, start, width = pieces[i - 1]
+                rests.append(blend_product(bt, start, width, cands[i - 1]))
+            if i >= 2:
+                bt, start, width = pieces[i - 2]
+                blend_and_store(bt, start, width, rests[i - 2])

@@ -60,7 +60,7 @@ def tile_anothergrucell_kernel(
             for s, source in enumerate((x_t, h_tm1)):
                 nc.sync.dma_start(
                     out=act_sb[s][:, first_bt : first_bt + 2, :],
-                    in_=source[first_bt * P : (first_bt + 2) * P, :].rearrange("(t p) k -> p t k", p=P),
+                    in_=source.rearrange("(p t) k -> p t k", t=BT)[:, first_bt : first_bt + 2, :],
                 )
 
         w_words = keep.tile([P, KC, 3 * WIDTH], U32, align_bytes=64)
@@ -224,7 +224,7 @@ def tile_anothergrucell_kernel(
             cols = slice(start, start + width)
             h_new = work.tile([P, N_TILE], F32, tag="h_new")
             nc.vector.tensor_tensor(out=h_new[:, :width], in0=uh_all[:, bt, cols], in1=rest, op=ALU.subtract)
-            nc.sync.dma_start(out=out[bt * P : (bt + 1) * P, cols], in_=h_new[:, :width])
+            nc.sync.dma_start(out=out.rearrange("(p t) n -> p t n", t=BT)[:, bt, cols], in_=h_new[:, :width])
 
         transpose_inputs(0)
         for bt in range(1, BT):
@@ -237,22 +237,17 @@ def tile_anothergrucell_kernel(
 
         for bt in range(BT):
             reset_gate(0, bt)
-        reset_gate(1, 0)
-        reset_gate(1, 1)
-        for bt in range(BT):
-            reset_times_h(0, bt)
-        reset_gate(1, 2)
-        reset_gate(1, 3)
-        reset_times_h(1, 0)
-        reset_times_h(1, 1)
-        update_gate(0, 0)
-        quantise_rh(0)
-        quantise_rh(1)
-        reset_times_h(1, 2)
-        reset_times_h(1, 3)
-        update_gate(0, 1)
-        quantise_rh(2)
-        quantise_rh(3)
+        for g in range(G):
+            for first_bt in range(0, BT, 2):
+                for bt in (first_bt, first_bt + 1):
+                    reset_times_h(g, bt)
+                for bt in (first_bt, first_bt + 1):
+                    if g == 0:
+                        reset_gate(1, bt)
+                    else:
+                        quantise_rh(bt)
+                if g == 1:
+                    update_gate(0, first_bt // 2)
 
         pieces = [(bt, nh * N_TILE, N_TILE) for bt in range(BT) for nh in range(NH)]
         pieces[-1:] = [(BT - 1, WIDTH - N_TILE, N_TILE // 2), (BT - 1, WIDTH - N_TILE // 2, N_TILE // 2)]

@@ -28,10 +28,6 @@ X, H = 0, 1
 FLOPS = 2 * BATCH * WIDTH * (3 * WIDTH + 2 * WIDTH + WIDTH)
 
 
-def by_byte_then_partition(ap):
-    return ap.rearrange("b (p t) -> b t p", t=PACK)
-
-
 def tile_anothergrucell_kernel(
     tc, x_t, h_tm1, iw_words, iw_scales, hw_words, hw_scales, bias, out
 ):
@@ -40,13 +36,14 @@ def tile_anothergrucell_kernel(
         ctx.enter_context(tc.manual_schedule())
         keep = ctx.enter_context(tc.tile_pool(name="keep", bufs=1))
         work = ctx.enter_context(tc.tile_pool(name="work", bufs=4))
-        psum_t = ctx.enter_context(tc.psum_pool(name="psum_t", bufs=3))
-        psum_acc = ctx.enter_context(tc.psum_pool(name="psum_acc", bufs=5))
+        psum = ctx.enter_context(tc.psum_pool(name="psum", bufs=8))
 
         bias_row = keep.tile([P, 3 * WIDTH], BF16)
         nc.vector.memset(bias_row[:].bitcast(I32), 0)
         nc.scalar.dma_start(out=bias_row[0:1, :], in_=bias.rearrange("(o n) -> o n", o=1))
-        w_planes = keep.tile([P, 3 * WIDTH], U8, align_bytes=64)
+        reset_planes_in = keep.tile([P, WIDTH], U8, align_bytes=64)
+        nc.vector.memset(reset_planes_in[:].bitcast(I32), 0)
+        w_planes = keep.tile([P, 2 * WIDTH], U8, align_bytes=64)
         nc.vector.memset(w_planes[:].bitcast(I32), 0)
         ones = keep.tile([P, P], BF16)
         nc.vector.memset(ones[:], 1.0)
@@ -56,97 +53,167 @@ def tile_anothergrucell_kernel(
         nc.scalar.activation(out=warm[:], in_=ones[:, 0:1], func=ACT.Sigmoid)
 
         act_sb = [keep.tile([P, BT, WIDTH], BF16, name="x_sb"), keep.tile([P, BT, WIDTH], BF16, name="h_sb")]
-        for first_bt in range(0, BT, 2):
-            for s, source in enumerate((x_t, h_tm1)):
-                nc.sync.dma_start(
-                    out=act_sb[s][:, first_bt : first_bt + 2, :],
-                    in_=source.rearrange("(p t) k -> p t k", t=BT)[:, first_bt : first_bt + 2, :],
-                )
+        reset_words_in = [
+            [keep.tile([P, G, N_TILE], U32, align_bytes=64, name="reset_words_in_%d%d" % (w, g)) for g in range(G)]
+            for w in (X, H)
+        ]
+        w_words = keep.tile([P, KC, 2 * WIDTH], U32, align_bytes=64)
 
-        w_words = keep.tile([P, KC, 3 * WIDTH], U32, align_bytes=64)
+        def load_activations(s, pair):
+            source = (x_t, h_tm1)[s]
+            nc.sync.dma_start(
+                out=act_sb[s][:, 2 * pair : 2 * pair + 2, :],
+                in_=source.rearrange("(p t) k -> p t k", t=BT)[:, 2 * pair : 2 * pair + 2, :],
+            )
 
-        def load_scale_columns(first, width):
+        def load_scale_columns(planes, first, width):
             for w, scales in enumerate((iw_scales, hw_scales)):
                 for q in range(4):
                     row = 32 * q + G * PACK * w
                     nc.sync.dma_start(
-                        out=w_planes[row : row + G * PACK, first : first + width].bitcast(I32),
+                        out=planes[row : row + G * PACK, :].bitcast(I32),
                         in_=scales[:, PACK * q : PACK * (q + 1), first : first + width].bitcast(I32),
                     )
 
-        def load_weight_columns(first, width):
-            for w, words in enumerate((iw_words, hw_words)):
-                nc.sync.dma_start(
-                    out=w_words[:, G * w : G * (w + 1), first : first + width].bitcast(I32),
-                    in_=words.rearrange("g p n t -> p g (n t)")[
-                        :, :, PACK * first : PACK * (first + width)
-                    ].bitcast(I32),
-                )
+        def load_words(tile_view, w, first, width):
+            words = (iw_words, hw_words)[w]
+            nc.sync.dma_start(
+                out=tile_view.bitcast(I32),
+                in_=words.rearrange("g p n t -> p g (n t)")[:, :, PACK * first : PACK * (first + width)].bitcast(I32),
+            )
 
-        load_scale_columns(RESET * WIDTH, WIDTH)
-        load_weight_columns(RESET * WIDTH, N_TILE)
-        load_weight_columns(RESET * WIDTH + N_TILE, N_TILE)
-        load_scale_columns(UPDATE * WIDTH, 2 * WIDTH)
-        load_weight_columns(UPDATE * WIDTH, WIDTH)
-        load_weight_columns(CAND * WIDTH, WIDTH)
+        load_activations(X, 0)
+        load_activations(H, 0)
+        load_activations(X, 1)
+        load_scale_columns(reset_planes_in, 0, WIDTH)
+        load_words(reset_words_in[X][0][:], X, 0, N_TILE)
+        load_activations(H, 1)
+        load_words(reset_words_in[H][0][:], H, 0, N_TILE)
+        load_words(reset_words_in[X][1][:], X, N_TILE, N_TILE)
+        load_words(reset_words_in[H][1][:], H, N_TILE, N_TILE)
+        load_scale_columns(w_planes, WIDTH, 2 * WIDTH)
+        for gate in (UPDATE, CAND):
+            for w in (X, H):
+                cols = slice((gate - 1) * WIDTH, gate * WIDTH)
+                load_words(w_words[:, G * w : G * (w + 1), cols], w, gate * WIDTH, WIDTH)
 
-        grouped = keep.tile([P, BT, KC, P, PACK], BF16, align_bytes=64)
-        act_codes = keep.tile([P, BT, KC, P], U32, align_bytes=64)
-        act_planes = keep.tile([P, BT, KC, P], U8, align_bytes=64)
+        grouped = keep.tile([P, KC, BT, P, PACK], BF16, align_bytes=64)
+        act_codes = keep.tile([P, KC, BT, P], U32, align_bytes=64)
+        act_planes = keep.tile([P, KC, BT, P], U8, align_bytes=64)
 
-        def transpose_inputs(bt):
-            for s in (X, H):
-                words = act_sb[s][:, bt, :].bitcast(F32)
-                bank = psum_t.tile([P, PACK, P], F32, tag="bank")
-                for g in range(G):
+        def transpose_inputs(s, pair):
+            for g in range(G):
+                bank = psum.tile([P, 2, 2, P], F32, tag="bank")
+                for j in range(2):
+                    words = act_sb[s][:, 2 * pair + j, :].bitcast(F32)
                     for half in range(2):
                         nc.tensor.transpose(
-                            out=bank[:, 2 * g + half, :],
+                            out=bank[:, j, half, :],
                             in_=words[:, g * K_PASS // 2 + half : (g + 1) * K_PASS // 2 : 2],
                             identity=ident[:],
                         )
                 nc.scalar.copy(
-                    out=grouped[:, bt, G * s : G * (s + 1), :, :].bitcast(F32),
-                    in_=bank[:].rearrange("p (g half) b -> p g b half", half=2),
+                    out=grouped[:, G * s + g, 2 * pair : 2 * pair + 2, :, :].bitcast(F32),
+                    in_=bank[:].rearrange("p j half b -> p j b half"),
                 )
 
-        def quantise_inputs(bt):
-            nc.vector.quantize_mx(
-                out=act_codes[:, bt].rearrange("p c b -> p (c b)").bitcast(FP8X4),
-                scales=act_planes[:, bt].rearrange("p c b -> p (c b)"),
-                in_=grouped[:, bt].rearrange("p c b t -> p (c b t)"),
+        def quantise_inputs(s, pair):
+            tiles = slice(2 * pair, 2 * pair + 2)
+            for kc in range(G * s, G * (s + 1)):
+                nc.vector.quantize_mx(
+                    out=act_codes[:, kc, tiles, :].rearrange("p j b -> p (j b)").bitcast(FP8X4),
+                    scales=act_planes[:, kc, tiles, :].rearrange("p j b -> p (j b)"),
+                    in_=grouped[:, kc, tiles, :, :].rearrange("p j b t -> p (j b t)"),
+                )
+
+        reset_words = keep.tile([P, KC, G, N_TILE], U32, align_bytes=64)
+        reset_planes = keep.tile([P, G, N_TILE], U8, align_bytes=64)
+
+        def permute_reset_planes(g):
+            nc.vector.tensor_copy(
+                out=reset_planes[:, g, :].rearrange("p (t m) -> p t m", t=PACK),
+                in_=reset_planes_in[:, g * N_TILE : (g + 1) * N_TILE].rearrange("p (m t) -> p t m", t=PACK),
             )
 
-        bias_bc = keep.tile([P, 3, WIDTH], F32)
+        def permute_reset_words(w, g):
+            for j in range(G):
+                nc.vector.tensor_copy(
+                    out=reset_words[:, G * w + j, g, :].bitcast(I32).rearrange("p (t c i) -> p c t i", t=PACK, i=4),
+                    in_=reset_words_in[w][g][:, j, :].bitcast(I32).rearrange("p (c i t) -> p c t i", t=PACK, i=4),
+                )
+
+        bias_bc = keep.tile([P, 2, WIDTH], F32)
 
         def broadcast_bias(gate):
             for nh in range(NH):
-                cols = slice(nh * N_TILE, (nh + 1) * N_TILE)
                 first = gate * WIDTH + nh * N_TILE
-                acc = psum_acc.tile([P, N_TILE], F32, tag="acc")
+                acc = psum.tile([P, N_TILE], F32, tag="bank")
                 nc.tensor.matmul(
                     out=acc[:], lhsT=ones[:], rhs=bias_row[:, first : first + N_TILE], start=True, stop=True
                 )
-                if gate == RESET:
-                    nc.vector.tensor_copy(
-                        out=bias_bc[:, gate, cols].rearrange("b (t p) -> b t p", t=PACK),
-                        in_=by_byte_then_partition(acc[:]),
-                    )
-                else:
-                    nc.vector.tensor_copy(out=bias_bc[:, gate, cols], in_=acc[:])
+                nc.scalar.copy(out=bias_bc[:, gate - UPDATE, nh * N_TILE : (nh + 1) * N_TILE], in_=acc[:])
 
-        rh_grouped = keep.tile([P, BT, G, P, PACK], BF16, align_bytes=64)
-        rh_codes = keep.tile([P, BT, G, P], U32, align_bytes=64)
-        rh_planes = keep.tile([P, BT, G, P], U8, align_bytes=64)
+        bias_r = keep.tile([P, G, PACK], F32)
+
+        def spread_reset_bias():
+            acc = psum.tile([P, G, PACK], F32, tag="bank")
+            for g in range(G):
+                for t in range(PACK):
+                    nc.tensor.matmul(
+                        out=acc[:, g, t : t + 1],
+                        lhsT=bias_row[:, g * N_TILE + t : (g + 1) * N_TILE : PACK],
+                        rhs=ones[:, 0:1],
+                        start=True,
+                        stop=True,
+                    )
+            nc.scalar.copy(out=bias_r[:], in_=acc[:])
+
+        rh_grouped = keep.tile([P, G, BT, P, PACK], BF16, align_bytes=64)
+        rh_codes = keep.tile([P, G, BT, P], U32, align_bytes=64)
+        rh_planes = keep.tile([P, G, BT, P], U8, align_bytes=64)
+        r_all = keep.tile([P, G, PACK, BATCH], F32)
+
+        def reset_pass(acc, g, t, kc):
+            cols = slice(t * P, (t + 1) * P)
+            nc.tensor.matmul_mx(
+                out=acc[:],
+                lhsT=reset_words[:, kc, g, cols].bitcast(FP8X4),
+                lhsT_scale=reset_planes[PACK * kc : P, g, cols],
+                rhs=act_codes[:, kc].rearrange("p j b -> p (j b)").bitcast(FP8X4),
+                rhs_scale=act_planes[:, kc].rearrange("p j b -> p (j b)"),
+                start=(kc == 0),
+                stop=(kc == KC - 1),
+            )
+
+        def reset_sigmoid(acc, g, t):
+            nc.scalar.activation(
+                out=r_all[:, g, t, :], in_=acc[:], func=ACT.Sigmoid, bias=bias_r[:, g, t : t + 1]
+            )
+
+        def reset_times_h(g, bt):
+            nc.vector.tensor_tensor(
+                out=rh_grouped[:, g, bt],
+                in0=r_all[:, g, :, bt * P : (bt + 1) * P].rearrange("p t b -> p b t"),
+                in1=grouped[:, G * H + g, bt],
+                op=ALU.mult,
+            )
+
+        def quantise_rh(g, first_bt, count):
+            tiles = slice(first_bt, first_bt + count)
+            nc.vector.quantize_mx(
+                out=rh_codes[:, g, tiles].rearrange("p j b -> p (j b)").bitcast(FP8X4),
+                scales=rh_planes[:, g, tiles].rearrange("p j b -> p (j b)"),
+                in_=rh_grouped[:, g, tiles].rearrange("p j b t -> p (j b t)"),
+            )
 
         def gate_sums(bt, gate, start, width):
-            first = gate * WIDTH + start
-            acc = psum_acc.tile([P, N_TILE], F32, tag="acc")
+            first = (gate - UPDATE) * WIDTH + start
+            acc = psum.tile([P, N_TILE], F32, tag="bank")
             for kc in range(KC):
                 if gate == CAND and kc >= G:
-                    codes, planes = rh_codes[:, bt, kc - G, :], rh_planes[:, bt, kc - G, :]
+                    codes, planes = rh_codes[:, kc - G, bt, :], rh_planes[:, kc - G, bt, :]
                 else:
-                    codes, planes = act_codes[:, bt, kc, :], act_planes[:, bt, kc, :]
+                    codes, planes = act_codes[:, kc, bt, :], act_planes[:, kc, bt, :]
                 nc.tensor.matmul_mx(
                     out=acc[:, :width],
                     lhsT=codes.bitcast(FP8X4),
@@ -158,43 +225,13 @@ def tile_anothergrucell_kernel(
                 )
             return acc[:, :width]
 
-        r_all = keep.tile([P, BT, G, PACK, P], F32)
-
-        def reset_gate(g, bt):
-            acc = gate_sums(bt, RESET, g * N_TILE, N_TILE)
-            nc.vector.tensor_tensor(
-                out=r_all[:, bt, g],
-                in0=by_byte_then_partition(acc),
-                in1=bias_bc[:, RESET, g * N_TILE : (g + 1) * N_TILE].rearrange("b (t p) -> b t p", t=PACK),
-                op=ALU.add,
-            )
-            nc.scalar.activation(out=r_all[:, bt, g], in_=r_all[:, bt, g], func=ACT.Sigmoid)
-
-        def reset_times_h(g, bt):
-            bank = psum_t.tile([P, PACK, P], F32, tag="bank")
-            for t in range(PACK):
-                nc.tensor.transpose(out=bank[:, t, :], in_=r_all[:, bt, g, t, :], identity=ident[:])
-            nc.vector.tensor_tensor(
-                out=rh_grouped[:, bt, g],
-                in0=bank[:].rearrange("p t b -> p b t"),
-                in1=grouped[:, bt, G * H + g],
-                op=ALU.mult,
-            )
-
-        def quantise_rh(bt):
-            nc.vector.quantize_mx(
-                out=rh_codes[:, bt].rearrange("p g b -> p (g b)").bitcast(FP8X4),
-                scales=rh_planes[:, bt].rearrange("p g b -> p (g b)"),
-                in_=rh_grouped[:, bt].rearrange("p g b t -> p (g b t)"),
-            )
-
         u_all = keep.tile([P, BT, WIDTH], F32)
         uh_all = keep.tile([P, BT, WIDTH], F32)
 
         def update_gate(bt, nh):
             cols = slice(nh * N_TILE, (nh + 1) * N_TILE)
             acc = gate_sums(bt, UPDATE, nh * N_TILE, N_TILE)
-            nc.vector.tensor_tensor(out=u_all[:, bt, cols], in0=acc, in1=bias_bc[:, UPDATE, cols], op=ALU.add)
+            nc.vector.tensor_tensor(out=u_all[:, bt, cols], in0=acc, in1=bias_bc[:, UPDATE - UPDATE, cols], op=ALU.add)
             nc.scalar.activation(out=u_all[:, bt, cols], in_=u_all[:, bt, cols], func=ACT.Sigmoid)
             nc.gpsimd.tensor_tensor(
                 out=uh_all[:, bt, cols], in0=u_all[:, bt, cols], in1=act_sb[H][:, bt, cols], op=ALU.mult
@@ -204,7 +241,7 @@ def tile_anothergrucell_kernel(
             cols = slice(start, start + width)
             acc = gate_sums(bt, CAND, start, width)
             cand = work.tile([P, N_TILE], F32, tag="cand")
-            nc.vector.tensor_tensor(out=cand[:, :width], in0=acc, in1=bias_bc[:, CAND, cols], op=ALU.add)
+            nc.vector.tensor_tensor(out=cand[:, :width], in0=acc, in1=bias_bc[:, CAND - UPDATE, cols], op=ALU.add)
             nc.scalar.activation(out=cand[:, :width], in_=cand[:, :width], func=ACT.Tanh)
             return cand[:, :width]
 
@@ -226,28 +263,49 @@ def tile_anothergrucell_kernel(
             nc.vector.tensor_tensor(out=h_new[:, :width], in0=uh_all[:, bt, cols], in1=rest, op=ALU.subtract)
             nc.sync.dma_start(out=out.rearrange("(p t) n -> p t n", t=BT)[:, bt, cols], in_=h_new[:, :width])
 
-        transpose_inputs(0)
-        for bt in range(1, BT):
-            transpose_inputs(bt)
-            quantise_inputs(bt - 1)
-        broadcast_bias(RESET)
-        quantise_inputs(BT - 1)
-        broadcast_bias(UPDATE)
-        broadcast_bias(CAND)
+        transpose_inputs(X, 0)
+        quantise_inputs(X, 0)
+        transpose_inputs(H, 0)
+        quantise_inputs(H, 0)
+        transpose_inputs(X, 1)
+        quantise_inputs(X, 1)
+        permute_reset_planes(0)
+        permute_reset_words(X, 0)
+        transpose_inputs(H, 1)
+        quantise_inputs(H, 1)
+        permute_reset_words(H, 0)
+        permute_reset_planes(1)
+        permute_reset_words(X, 1)
+        permute_reset_words(H, 1)
+        spread_reset_bias()
+        for gate in (UPDATE, CAND):
+            broadcast_bias(gate)
 
+        sums = []
+        for t in range(PACK):
+            acc = psum.tile([P, BATCH], F32, tag="bank")
+            sums.append(acc)
+            for kc in range(G):
+                reset_pass(acc, 0, t, kc)
+        for t in range(PACK):
+            for kc in range(G, KC):
+                reset_pass(sums[t], 0, t, kc)
+            reset_sigmoid(sums[t], 0, t)
+        for t in range(PACK):
+            acc = psum.tile([P, BATCH], F32, tag="bank")
+            for kc in range(KC):
+                reset_pass(acc, 1, t, kc)
+            reset_sigmoid(acc, 1, t)
         for bt in range(BT):
-            reset_gate(0, bt)
-        for g in range(G):
-            for first_bt in range(0, BT, 2):
-                for bt in (first_bt, first_bt + 1):
-                    reset_times_h(g, bt)
-                for bt in (first_bt, first_bt + 1):
-                    if g == 0:
-                        reset_gate(1, bt)
-                    else:
-                        quantise_rh(bt)
-                if g == 1:
-                    update_gate(0, first_bt // 2)
+            reset_times_h(0, bt)
+        quantise_rh(0, 0, BT)
+        reset_times_h(1, 0)
+        for bt in range(1, BT):
+            reset_times_h(1, bt)
+            quantise_rh(1, bt - 1, 1)
+            if bt <= NH:
+                update_gate(0, bt - 1)
+        quantise_rh(1, BT - 1, 1)
 
         pieces = [(bt, nh * N_TILE, N_TILE) for bt in range(BT) for nh in range(NH)]
         pieces[-1:] = [(BT - 1, WIDTH - N_TILE, N_TILE // 2), (BT - 1, WIDTH - N_TILE // 2, N_TILE // 2)]

@@ -85,9 +85,9 @@ def tile_anothergrucell_kernel(
         load_activations(X, 0)
         load_activations(H, 0)
         load_activations(X, 1)
+        load_activations(H, 1)
         load_scale_columns(reset_planes_in, 0, WIDTH)
         load_words(reset_words_in[X][0][:], X, 0, N_TILE)
-        load_activations(H, 1)
         load_words(reset_words_in[H][0][:], H, 0, N_TILE)
         load_words(reset_words_in[X][1][:], X, N_TILE, N_TILE)
         load_words(reset_words_in[H][1][:], H, N_TILE, N_TILE)

@@ -22,6 +22,7 @@ G = WIDTH // K_PASS
 KC = 2 * G
 N_TILE = 512
 NH = WIDTH // N_TILE
+CT = WIDTH // P
 RESET, UPDATE, CAND = 0, 1, 2
 X, H = 0, 1
 
@@ -41,9 +42,7 @@ def tile_anothergrucell_kernel(
         bias_row = keep.tile([P, 3 * WIDTH], BF16)
         nc.vector.memset(bias_row[:].bitcast(I32), 0)
         nc.scalar.dma_start(out=bias_row[0:1, :], in_=bias.rearrange("(o n) -> o n", o=1))
-        reset_planes_in = keep.tile([P, WIDTH], U8, align_bytes=64)
-        nc.vector.memset(reset_planes_in[:].bitcast(I32), 0)
-        w_planes = keep.tile([P, 2 * WIDTH], U8, align_bytes=64)
+        w_planes = keep.tile([P, 3 * WIDTH], U8, align_bytes=64)
         nc.vector.memset(w_planes[:].bitcast(I32), 0)
         ones = keep.tile([P, P], BF16)
         nc.vector.memset(ones[:], 1.0)
@@ -66,14 +65,14 @@ def tile_anothergrucell_kernel(
                 in_=source.rearrange("(p t) k -> p t k", t=BT)[:, 2 * pair : 2 * pair + 2, :],
             )
 
-        def load_scale_columns(planes, first, width):
-            for w, scales in enumerate((iw_scales, hw_scales)):
-                for q in range(4):
-                    row = 32 * q + G * PACK * w
-                    nc.sync.dma_start(
-                        out=planes[row : row + G * PACK, :].bitcast(I32),
-                        in_=scales[:, PACK * q : PACK * (q + 1), first : first + width].bitcast(I32),
-                    )
+        def load_scales(w):
+            scales = (iw_scales, hw_scales)[w]
+            for q in range(4):
+                row = 32 * q + G * PACK * w
+                nc.sync.dma_start(
+                    out=w_planes[row : row + G * PACK, :].bitcast(I32),
+                    in_=scales[:, PACK * q : PACK * (q + 1), :].bitcast(I32),
+                )
 
         def load_words(tile_view, w, first, width):
             words = (iw_words, hw_words)[w]
@@ -85,17 +84,17 @@ def tile_anothergrucell_kernel(
         load_activations(X, 0)
         load_activations(H, 0)
         load_activations(X, 1)
+        load_scales(X)
         load_activations(H, 1)
-        load_scale_columns(reset_planes_in, 0, WIDTH)
-        load_words(reset_words_in[X][0][:], X, 0, N_TILE)
-        load_words(reset_words_in[H][0][:], H, 0, N_TILE)
-        load_words(reset_words_in[X][1][:], X, N_TILE, N_TILE)
-        load_words(reset_words_in[H][1][:], H, N_TILE, N_TILE)
-        load_scale_columns(w_planes, WIDTH, 2 * WIDTH)
-        for gate in (UPDATE, CAND):
+        load_scales(H)
+        for g in range(G):
             for w in (X, H):
-                cols = slice((gate - 1) * WIDTH, gate * WIDTH)
-                load_words(w_words[:, G * w : G * (w + 1), cols], w, gate * WIDTH, WIDTH)
+                load_words(reset_words_in[w][g][:], w, g * N_TILE, N_TILE)
+        for gate in (UPDATE, CAND):
+            for nh in range(NH):
+                for w in (X, H):
+                    first = (gate - UPDATE) * WIDTH + nh * N_TILE
+                    load_words(w_words[:, G * w : G * (w + 1), first : first + N_TILE], w, WIDTH + first, N_TILE)
 
         grouped = keep.tile([P, KC, BT, P, PACK], BF16, align_bytes=64)
         act_codes = keep.tile([P, KC, BT, P], U32, align_bytes=64)
@@ -132,7 +131,7 @@ def tile_anothergrucell_kernel(
         def permute_reset_planes(g):
             nc.vector.tensor_copy(
                 out=reset_planes[:, g, :].rearrange("p (t m) -> p t m", t=PACK),
-                in_=reset_planes_in[:, g * N_TILE : (g + 1) * N_TILE].rearrange("p (m t) -> p t m", t=PACK),
+                in_=w_planes[:, g * N_TILE : (g + 1) * N_TILE].rearrange("p (m t) -> p t m", t=PACK),
             )
 
         def permute_reset_words(w, g):
@@ -142,31 +141,51 @@ def tile_anothergrucell_kernel(
                     in_=reset_words_in[w][g][:, j, :].bitcast(I32).rearrange("p (c i t) -> p c t i", t=PACK, i=4),
                 )
 
-        bias_bc = keep.tile([P, 2, WIDTH], F32)
+        bias_u = keep.tile([P, WIDTH], F32)
 
-        def broadcast_bias(gate):
+        def broadcast_update_bias():
             for nh in range(NH):
-                first = gate * WIDTH + nh * N_TILE
+                first = UPDATE * WIDTH + nh * N_TILE
                 acc = psum.tile([P, N_TILE], F32, tag="bank")
                 nc.tensor.matmul(
                     out=acc[:], lhsT=ones[:], rhs=bias_row[:, first : first + N_TILE], start=True, stop=True
                 )
-                nc.scalar.copy(out=bias_bc[:, gate - UPDATE, nh * N_TILE : (nh + 1) * N_TILE], in_=acc[:])
+                nc.scalar.copy(out=bias_u[:, nh * N_TILE : (nh + 1) * N_TILE], in_=acc[:])
+
+        bias_cand = keep.tile([P, N_TILE], F32)
+
+        def broadcast_candidate_bias():
+            acc = psum.tile([P, N_TILE], F32, tag="bank")
+            nc.tensor.matmul(
+                out=acc[:],
+                lhsT=ones[:],
+                rhs=bias_row[:, CAND * WIDTH : CAND * WIDTH + N_TILE],
+                start=True,
+                stop=True,
+            )
+            nc.scalar.copy(out=bias_cand[:], in_=acc[:])
 
         bias_r = keep.tile([P, G, PACK], F32)
+        bias_c = keep.tile([P, CT], F32)
 
-        def spread_reset_bias():
-            acc = psum.tile([P, G, PACK], F32, tag="bank")
-            for g in range(G):
-                for t in range(PACK):
-                    nc.tensor.matmul(
-                        out=acc[:, g, t : t + 1],
-                        lhsT=bias_row[:, g * N_TILE + t : (g + 1) * N_TILE : PACK],
-                        rhs=ones[:, 0:1],
-                        start=True,
-                        stop=True,
-                    )
-            nc.scalar.copy(out=bias_r[:], in_=acc[:])
+        def spread_bias():
+            acc = psum.tile([P, 2, CT], F32, tag="bank")
+            for j in range(CT):
+                first = (j // PACK) * N_TILE + j % PACK
+                nc.tensor.matmul(
+                    out=acc[:, 0, j : j + 1],
+                    lhsT=bias_row[:, first : first + N_TILE - PACK + 1 : PACK],
+                    rhs=ones[:, 0:1],
+                    start=True,
+                    stop=True,
+                )
+            for j in range(CT):
+                first = CAND * WIDTH + j * P
+                nc.tensor.matmul(
+                    out=acc[:, 1, j : j + 1], lhsT=bias_row[:, first : first + P], rhs=ones[:, 0:1], start=True, stop=True
+                )
+            nc.scalar.copy(out=bias_r[:].rearrange("p g t -> p (g t)"), in_=acc[:, 0, :])
+            nc.scalar.copy(out=bias_c[:], in_=acc[:, 1, :])
 
         rh_grouped = keep.tile([P, G, BT, P, PACK], BF16, align_bytes=64)
         rh_codes = keep.tile([P, G, BT, P], U32, align_bytes=64)
@@ -206,8 +225,11 @@ def tile_anothergrucell_kernel(
                 in_=rh_grouped[:, g, tiles].rearrange("p j b t -> p (j b t)"),
             )
 
-        def gate_sums(bt, gate, start, width):
-            first = (gate - UPDATE) * WIDTH + start
+        u_all = keep.tile([P, BT, WIDTH], F32)
+        uh_all = keep.tile([P, BT, WIDTH], F32)
+
+        def row_sums(bt, gate, nh):
+            first = (gate - UPDATE) * WIDTH + nh * N_TILE
             acc = psum.tile([P, N_TILE], F32, tag="bank")
             for kc in range(KC):
                 if gate == CAND and kc >= G:
@@ -215,55 +237,95 @@ def tile_anothergrucell_kernel(
                 else:
                     codes, planes = act_codes[:, kc, bt, :], act_planes[:, kc, bt, :]
                 nc.tensor.matmul_mx(
-                    out=acc[:, :width],
+                    out=acc[:],
                     lhsT=codes.bitcast(FP8X4),
                     lhsT_scale=planes,
-                    rhs=w_words[:, kc, first : first + width].bitcast(FP8X4),
-                    rhs_scale=w_planes[PACK * kc : P, first : first + width],
+                    rhs=w_words[:, kc, first : first + N_TILE].bitcast(FP8X4),
+                    rhs_scale=w_planes[PACK * kc : P, WIDTH + first : WIDTH + first + N_TILE],
                     start=(kc == 0),
                     stop=(kc == KC - 1),
                 )
-            return acc[:, :width]
-
-        u_all = keep.tile([P, BT, WIDTH], F32)
-        uh_all = keep.tile([P, BT, WIDTH], F32)
+            return acc
 
         def update_gate(bt, nh):
             cols = slice(nh * N_TILE, (nh + 1) * N_TILE)
-            acc = gate_sums(bt, UPDATE, nh * N_TILE, N_TILE)
-            nc.vector.tensor_tensor(out=u_all[:, bt, cols], in0=acc, in1=bias_bc[:, UPDATE - UPDATE, cols], op=ALU.add)
+            acc = row_sums(bt, UPDATE, nh)
+            nc.vector.tensor_tensor(out=u_all[:, bt, cols], in0=acc[:], in1=bias_u[:, cols], op=ALU.add)
             nc.scalar.activation(out=u_all[:, bt, cols], in_=u_all[:, bt, cols], func=ACT.Sigmoid)
             nc.gpsimd.tensor_tensor(
                 out=uh_all[:, bt, cols], in0=u_all[:, bt, cols], in1=act_sb[H][:, bt, cols], op=ALU.mult
             )
 
-        def candidate(bt, start, width):
-            cols = slice(start, start + width)
-            acc = gate_sums(bt, CAND, start, width)
-            cand = work.tile([P, N_TILE], F32, tag="cand")
-            nc.vector.tensor_tensor(out=cand[:, :width], in0=acc, in1=bias_bc[:, CAND - UPDATE, cols], op=ALU.add)
-            nc.scalar.activation(out=cand[:, :width], in_=cand[:, :width], func=ACT.Tanh)
-            return cand[:, :width]
+        def candidate(j, first_bt, count):
+            tiles = slice(first_bt, first_bt + count)
+            cols = slice(WIDTH + j * P, WIDTH + (j + 1) * P)
+            plane_cols = slice(CAND * WIDTH + j * P, CAND * WIDTH + (j + 1) * P)
+            acc = psum.tile([P, BATCH], F32, tag="bank")
+            for kc in range(KC):
+                codes, planes = (act_codes[:, kc], act_planes[:, kc]) if kc < G else (rh_codes[:, kc - G], rh_planes[:, kc - G])
+                nc.tensor.matmul_mx(
+                    out=acc[:, : count * P],
+                    lhsT=w_words[:, kc, cols].bitcast(FP8X4),
+                    lhsT_scale=w_planes[PACK * kc : P, plane_cols],
+                    rhs=codes[:, tiles].rearrange("p j b -> p (j b)").bitcast(FP8X4),
+                    rhs_scale=planes[:, tiles].rearrange("p j b -> p (j b)"),
+                    start=(kc == 0),
+                    stop=(kc == KC - 1),
+                )
+            cand = work.tile([P, BT, P], F32, tag="cand")
+            nc.scalar.activation(
+                out=cand[:, :count].rearrange("p j b -> p (j b)"),
+                in_=acc[:, : count * P],
+                func=ACT.Tanh,
+                bias=bias_c[:, j : j + 1],
+            )
+            return cand
 
-        def blend_product(bt, start, width, cand):
-            rest = work.tile([P, N_TILE], F32, tag="rest")
+        def candidate_rows(bt):
+            acc = row_sums(bt, CAND, 0)
+            cand = work.tile([P, N_TILE], F32, tag="cand_rows")
+            nc.vector.tensor_tensor(out=cand[:], in0=acc[:], in1=bias_cand[:], op=ALU.add)
+            nc.scalar.activation(out=cand[:], in_=cand[:], func=ACT.Tanh)
+            return cand
+
+        def transpose_candidate(count, cand):
+            bank = psum.tile([P, BT, P], F32, tag="bank")
+            for i in range(count):
+                nc.tensor.transpose(out=bank[:, i, :], in_=cand[:, i, :], identity=ident[:])
+            return bank
+
+        def blend_product(j, first_bt, count, bank):
+            if count == 0:
+                rest = work.tile([P, N_TILE], F32, tag="rest_rows")
+                nc.vector.scalar_tensor_tensor(
+                    out=rest[:], in0=u_all[:, j, :N_TILE], scalar=1.0, in1=bank[:], op0=ALU.subtract, op1=ALU.mult
+                )
+                return rest
+            rest = work.tile([P, BT, P], F32, tag="rest")
             nc.vector.scalar_tensor_tensor(
-                out=rest[:, :width],
-                in0=u_all[:, bt, start : start + width],
+                out=rest[:, :count],
+                in0=u_all[:, first_bt : first_bt + count, j * P : (j + 1) * P],
                 scalar=1.0,
-                in1=cand,
+                in1=bank[:, :count],
                 op0=ALU.subtract,
                 op1=ALU.mult,
             )
-            return rest[:, :width]
+            return rest
 
-        def blend_and_store(bt, start, width, rest):
-            cols = slice(start, start + width)
-            h_new = work.tile([P, N_TILE], F32, tag="h_new")
-            nc.vector.tensor_tensor(out=h_new[:, :width], in0=uh_all[:, bt, cols], in1=rest, op=ALU.subtract)
-            nc.sync.dma_start(out=out.rearrange("(p t) n -> p t n", t=BT)[:, bt, cols], in_=h_new[:, :width])
+        def blend_and_store(j, first_bt, count, rest):
+            if count == 0:
+                h_new = work.tile([P, N_TILE], F32, tag="h_new_rows")
+                nc.vector.tensor_tensor(out=h_new[:], in0=uh_all[:, j, :N_TILE], in1=rest[:], op=ALU.subtract)
+                nc.sync.dma_start(out=out.rearrange("(p t) n -> p t n", t=BT)[:, j, :N_TILE], in_=h_new[:])
+                return
+            tiles = slice(first_bt, first_bt + count)
+            cols = slice(j * P, (j + 1) * P)
+            h_new = work.tile([P, BT, P], F32, tag="h_new")
+            nc.vector.tensor_tensor(out=h_new[:, :count], in0=uh_all[:, tiles, cols], in1=rest[:, :count], op=ALU.subtract)
+            nc.sync.dma_start(out=out.rearrange("(p t) n -> p t n", t=BT)[:, tiles, cols], in_=h_new[:, :count])
 
         transpose_inputs(X, 0)
+        spread_bias()
         quantise_inputs(X, 0)
         transpose_inputs(H, 0)
         quantise_inputs(H, 0)
@@ -272,14 +334,13 @@ def tile_anothergrucell_kernel(
         permute_reset_planes(0)
         permute_reset_words(X, 0)
         transpose_inputs(H, 1)
+        broadcast_update_bias()
+        broadcast_candidate_bias()
         quantise_inputs(H, 1)
         permute_reset_words(H, 0)
         permute_reset_planes(1)
-        permute_reset_words(X, 1)
-        permute_reset_words(H, 1)
-        spread_reset_bias()
-        for gate in (UPDATE, CAND):
-            broadcast_bias(gate)
+        for w in (X, H):
+            permute_reset_words(w, 1)
 
         sums = []
         for t in range(PACK):
@@ -303,23 +364,31 @@ def tile_anothergrucell_kernel(
         for bt in range(1, BT):
             reset_times_h(1, bt)
             quantise_rh(1, bt - 1, 1)
-            if bt <= NH:
-                update_gate(0, bt - 1)
+        update_gate(0, 0)
         quantise_rh(1, BT - 1, 1)
+        for bt in range(1, BT):
+            update_gate(bt, 0)
 
-        pieces = [(bt, nh * N_TILE, N_TILE) for bt in range(BT) for nh in range(NH)]
-        pieces[-1:] = [(BT - 1, WIDTH - N_TILE, N_TILE // 2), (BT - 1, WIDTH - N_TILE // 2, N_TILE // 2)]
+        H_ROWS = [("rows", bt) for bt in range(BT)]
+        pieces = H_ROWS + [(j, 0, BT) for j in range(PACK, CT - 1)] + [(CT - 1, 0, BT // 2), (CT - 1, BT // 2, BT // 2)]
         cands = []
         rests = []
         for i in range(len(pieces) + 2):
             if i < len(pieces):
-                bt, start, width = pieces[i]
-                cands.append(candidate(bt, start, width))
-                if bt + 1 < BT:
-                    update_gate(bt + 1, start // N_TILE)
+                if i < BT:
+                    cands.append(candidate_rows(i))
+                    update_gate(i, 1)
+                else:
+                    cands.append(candidate(*pieces[i]))
             if 1 <= i <= len(pieces):
-                bt, start, width = pieces[i - 1]
-                rests.append(blend_product(bt, start, width, cands[i - 1]))
+                if i - 1 < BT:
+                    rests.append(blend_product(i - 1, 0, 0, cands[i - 1]))
+                else:
+                    j, first_bt, count = pieces[i - 1]
+                    bank = transpose_candidate(count, cands[i - 1])
+                    rests.append(blend_product(j, first_bt, count, bank))
             if i >= 2:
-                bt, start, width = pieces[i - 2]
-                blend_and_store(bt, start, width, rests[i - 2])
+                if i - 2 < BT:
+                    blend_and_store(i - 2, 0, 0, rests[i - 2])
+                else:
+                    blend_and_store(*pieces[i - 2], rests[i - 2])

@@ -42,7 +42,9 @@ def tile_anothergrucell_kernel(
         bias_row = keep.tile([P, 3 * WIDTH], BF16)
         nc.vector.memset(bias_row[:].bitcast(I32), 0)
         nc.scalar.dma_start(out=bias_row[0:1, :], in_=bias.rearrange("(o n) -> o n", o=1))
-        w_planes = keep.tile([P, 3 * WIDTH], U8, align_bytes=64)
+        reset_planes_in = keep.tile([P, WIDTH], U8, align_bytes=64)
+        nc.vector.memset(reset_planes_in[:].bitcast(I32), 0)
+        w_planes = keep.tile([P, 2 * WIDTH], U8, align_bytes=64)
         nc.vector.memset(w_planes[:].bitcast(I32), 0)
         ones = keep.tile([P, P], BF16)
         nc.vector.memset(ones[:], 1.0)
@@ -65,14 +67,14 @@ def tile_anothergrucell_kernel(
                 in_=source.rearrange("(p t) k -> p t k", t=BT)[:, 2 * pair : 2 * pair + 2, :],
             )
 
-        def load_scales(w):
-            scales = (iw_scales, hw_scales)[w]
-            for q in range(4):
-                row = 32 * q + G * PACK * w
-                nc.sync.dma_start(
-                    out=w_planes[row : row + G * PACK, :].bitcast(I32),
-                    in_=scales[:, PACK * q : PACK * (q + 1), :].bitcast(I32),
-                )
+        def load_scale_columns(planes, first, width):
+            for w, scales in enumerate((iw_scales, hw_scales)):
+                for q in range(4):
+                    row = 32 * q + G * PACK * w
+                    nc.sync.dma_start(
+                        out=planes[row : row + G * PACK, :].bitcast(I32),
+                        in_=scales[:, PACK * q : PACK * (q + 1), first : first + width].bitcast(I32),
+                    )
 
         def load_words(tile_view, w, first, width):
             words = (iw_words, hw_words)[w]
@@ -81,20 +83,18 @@ def tile_anothergrucell_kernel(
                 in_=words.rearrange("g p n t -> p g (n t)")[:, :, PACK * first : PACK * (first + width)].bitcast(I32),
             )
 
-        load_activations(X, 0)
-        load_activations(H, 0)
-        load_activations(X, 1)
-        load_scales(X)
-        load_activations(H, 1)
-        load_scales(H)
+        for pair in range(2):
+            for s in (X, H):
+                load_activations(s, pair)
+        load_scale_columns(reset_planes_in, 0, WIDTH)
         for g in range(G):
             for w in (X, H):
                 load_words(reset_words_in[w][g][:], w, g * N_TILE, N_TILE)
+        load_scale_columns(w_planes, WIDTH, 2 * WIDTH)
         for gate in (UPDATE, CAND):
-            for nh in range(NH):
-                for w in (X, H):
-                    first = (gate - UPDATE) * WIDTH + nh * N_TILE
-                    load_words(w_words[:, G * w : G * (w + 1), first : first + N_TILE], w, WIDTH + first, N_TILE)
+            for w in (X, H):
+                first = (gate - UPDATE) * WIDTH
+                load_words(w_words[:, G * w : G * (w + 1), first : first + WIDTH], w, WIDTH + first, WIDTH)
 
         grouped = keep.tile([P, KC, BT, P, PACK], BF16, align_bytes=64)
         act_codes = keep.tile([P, KC, BT, P], U32, align_bytes=64)
@@ -131,7 +131,7 @@ def tile_anothergrucell_kernel(
         def permute_reset_planes(g):
             nc.vector.tensor_copy(
                 out=reset_planes[:, g, :].rearrange("p (t m) -> p t m", t=PACK),
-                in_=w_planes[:, g * N_TILE : (g + 1) * N_TILE].rearrange("p (m t) -> p t m", t=PACK),
+                in_=reset_planes_in[:, g * N_TILE : (g + 1) * N_TILE].rearrange("p (m t) -> p t m", t=PACK),
             )
 
         def permute_reset_words(w, g):
@@ -241,7 +241,7 @@ def tile_anothergrucell_kernel(
                     lhsT=codes.bitcast(FP8X4),
                     lhsT_scale=planes,
                     rhs=w_words[:, kc, first : first + N_TILE].bitcast(FP8X4),
-                    rhs_scale=w_planes[PACK * kc : P, WIDTH + first : WIDTH + first + N_TILE],
+                    rhs_scale=w_planes[PACK * kc : P, first : first + N_TILE],
                     start=(kc == 0),
                     stop=(kc == KC - 1),
                 )
@@ -259,14 +259,13 @@ def tile_anothergrucell_kernel(
         def candidate(j, first_bt, count):
             tiles = slice(first_bt, first_bt + count)
             cols = slice(WIDTH + j * P, WIDTH + (j + 1) * P)
-            plane_cols = slice(CAND * WIDTH + j * P, CAND * WIDTH + (j + 1) * P)
             acc = psum.tile([P, BATCH], F32, tag="bank")
             for kc in range(KC):
                 codes, planes = (act_codes[:, kc], act_planes[:, kc]) if kc < G else (rh_codes[:, kc - G], rh_planes[:, kc - G])
                 nc.tensor.matmul_mx(
                     out=acc[:, : count * P],
                     lhsT=w_words[:, kc, cols].bitcast(FP8X4),
-                    lhsT_scale=w_planes[PACK * kc : P, plane_cols],
+                    lhsT_scale=w_planes[PACK * kc : P, cols],
                     rhs=codes[:, tiles].rearrange("p j b -> p (j b)").bitcast(FP8X4),
                     rhs_scale=planes[:, tiles].rearrange("p j b -> p (j b)"),
                     start=(kc == 0),

@@ -39,15 +39,14 @@ def tile_anothergrucell_kernel(
         work = ctx.enter_context(tc.tile_pool(name="work", bufs=4))
         psum = ctx.enter_context(tc.psum_pool(name="psum", bufs=8))
 
-        bias_row = keep.tile([P, 3 * WIDTH], BF16)
-        nc.vector.memset(bias_row[:].bitcast(I32), 0)
-        nc.scalar.dma_start(out=bias_row[0:1, :], in_=bias.rearrange("(o n) -> o n", o=1))
         reset_planes_in = keep.tile([P, WIDTH], U8, align_bytes=64)
         nc.vector.memset(reset_planes_in[:].bitcast(I32), 0)
-        w_planes = keep.tile([P, 2 * WIDTH], U8, align_bytes=64)
-        nc.vector.memset(w_planes[:].bitcast(I32), 0)
         ones = keep.tile([P, P], BF16)
         nc.vector.memset(ones[:], 1.0)
+        bias_row = keep.tile([P, 3 * WIDTH], BF16)
+        nc.vector.memset(bias_row[:].bitcast(I32), 0)
+        w_planes = keep.tile([P, 2 * WIDTH], U8, align_bytes=64)
+        nc.vector.memset(w_planes[:].bitcast(I32), 0)
         ident = keep.tile([P, P], F32)
         make_identity(nc, ident[:])
         warm = keep.tile([P, 1], F32)
@@ -67,14 +66,14 @@ def tile_anothergrucell_kernel(
                 in_=source.rearrange("(p t) k -> p t k", t=BT)[:, 2 * pair : 2 * pair + 2, :],
             )
 
-        def load_scale_columns(planes, first, width):
-            for w, scales in enumerate((iw_scales, hw_scales)):
-                for q in range(4):
-                    row = 32 * q + G * PACK * w
-                    nc.sync.dma_start(
-                        out=planes[row : row + G * PACK, :].bitcast(I32),
-                        in_=scales[:, PACK * q : PACK * (q + 1), first : first + width].bitcast(I32),
-                    )
+        def load_scale_columns(planes, w, first, width):
+            scales = (iw_scales, hw_scales)[w]
+            for q in range(4):
+                row = 32 * q + G * PACK * w
+                nc.sync.dma_start(
+                    out=planes[row : row + G * PACK, :].bitcast(I32),
+                    in_=scales[:, PACK * q : PACK * (q + 1), first : first + width].bitcast(I32),
+                )
 
         def load_words(tile_view, w, first, width):
             words = (iw_words, hw_words)[w]
@@ -83,14 +82,17 @@ def tile_anothergrucell_kernel(
                 in_=words.rearrange("g p n t -> p g (n t)")[:, :, PACK * first : PACK * (first + width)].bitcast(I32),
             )
 
+        load_scale_columns(reset_planes_in, X, 0, WIDTH)
         for pair in range(2):
             for s in (X, H):
                 load_activations(s, pair)
-        load_scale_columns(reset_planes_in, 0, WIDTH)
+        nc.scalar.dma_start(out=bias_row[0:1, :], in_=bias.rearrange("(o n) -> o n", o=1))
+        load_scale_columns(reset_planes_in, H, 0, WIDTH)
         for g in range(G):
             for w in (X, H):
                 load_words(reset_words_in[w][g][:], w, g * N_TILE, N_TILE)
-        load_scale_columns(w_planes, WIDTH, 2 * WIDTH)
+        for w in (X, H):
+            load_scale_columns(w_planes, w, WIDTH, 2 * WIDTH)
         for gate in (UPDATE, CAND):
             for w in (X, H):
                 first = (gate - UPDATE) * WIDTH
@@ -324,7 +326,6 @@ def tile_anothergrucell_kernel(
             nc.sync.dma_start(out=out.rearrange("(p t) n -> p t n", t=BT)[:, tiles, cols], in_=h_new[:, :count])
 
         transpose_inputs(X, 0)
-        spread_bias()
         quantise_inputs(X, 0)
         transpose_inputs(H, 0)
         quantise_inputs(H, 0)
@@ -333,6 +334,7 @@ def tile_anothergrucell_kernel(
         permute_reset_planes(0)
         permute_reset_words(X, 0)
         transpose_inputs(H, 1)
+        spread_bias()
         broadcast_update_bias()
         broadcast_candidate_bias()
         quantise_inputs(H, 1)

@@ -39,18 +39,21 @@ def tile_anothergrucell_kernel(
         work = ctx.enter_context(tc.tile_pool(name="work", bufs=4))
         psum = ctx.enter_context(tc.psum_pool(name="psum", bufs=8))
 
+        warm = keep.tile([P, 1], F32)
+        nc.vector.memset(warm[:], 0.0)
+        bias_rows = keep.tile([P, P], BF16)
+        nc.vector.memset(bias_rows[:].bitcast(I32), 0)
+        bias_reset_row = keep.tile([P, WIDTH], BF16)
+        nc.vector.memset(bias_reset_row[:].bitcast(I32), 0)
         reset_planes_in = keep.tile([P, WIDTH], U8, align_bytes=64)
         nc.vector.memset(reset_planes_in[:].bitcast(I32), 0)
-        ones = keep.tile([P, P], BF16)
-        nc.vector.memset(ones[:], 1.0)
-        bias_row = keep.tile([P, 3 * WIDTH], BF16)
-        nc.vector.memset(bias_row[:].bitcast(I32), 0)
         w_planes = keep.tile([P, 2 * WIDTH], U8, align_bytes=64)
         nc.vector.memset(w_planes[:].bitcast(I32), 0)
         ident = keep.tile([P, P], F32)
         make_identity(nc, ident[:])
-        warm = keep.tile([P, 1], F32)
-        nc.scalar.activation(out=warm[:], in_=ones[:, 0:1], func=ACT.Sigmoid)
+        ident_bf = keep.tile([P, P], BF16)
+        nc.vector.tensor_copy(out=ident_bf[:], in_=ident[:])
+        nc.scalar.activation(out=warm[:], in_=warm[:], func=ACT.Sigmoid)
 
         act_sb = [keep.tile([P, BT, WIDTH], BF16, name="x_sb"), keep.tile([P, BT, WIDTH], BF16, name="h_sb")]
         reset_words_in = [
@@ -82,15 +85,18 @@ def tile_anothergrucell_kernel(
                 in_=words.rearrange("g p n t -> p g (n t)")[:, :, PACK * first : PACK * (first + width)].bitcast(I32),
             )
 
+        load_activations(X, 0)
+        nc.sync.dma_start(out=bias_rows[: 2 * CT, :], in_=bias[WIDTH:].rearrange("(j n) -> j n", n=P))
+        nc.sync.dma_start(out=bias_reset_row[0:1, :], in_=bias[:WIDTH].rearrange("(o n) -> o n", o=1))
+        load_activations(H, 0)
+        load_activations(X, 1)
         load_scale_columns(reset_planes_in, X, 0, WIDTH)
-        for pair in range(2):
-            for s in (X, H):
-                load_activations(s, pair)
-        nc.scalar.dma_start(out=bias_row[0:1, :], in_=bias.rearrange("(o n) -> o n", o=1))
+        load_activations(H, 1)
+        load_words(reset_words_in[X][0][:], X, 0, N_TILE)
         load_scale_columns(reset_planes_in, H, 0, WIDTH)
-        for g in range(G):
-            for w in (X, H):
-                load_words(reset_words_in[w][g][:], w, g * N_TILE, N_TILE)
+        load_words(reset_words_in[H][0][:], H, 0, N_TILE)
+        for w in (X, H):
+            load_words(reset_words_in[w][1][:], w, N_TILE, N_TILE)
         for w in (X, H):
             load_scale_columns(w_planes, w, WIDTH, 2 * WIDTH)
         for gate in (UPDATE, CAND):
@@ -144,50 +150,42 @@ def tile_anothergrucell_kernel(
                 )
 
         bias_u = keep.tile([P, WIDTH], F32)
-
-        def broadcast_update_bias():
-            for nh in range(NH):
-                first = UPDATE * WIDTH + nh * N_TILE
-                acc = psum.tile([P, N_TILE], F32, tag="bank")
-                nc.tensor.matmul(
-                    out=acc[:], lhsT=ones[:], rhs=bias_row[:, first : first + N_TILE], start=True, stop=True
-                )
-                nc.scalar.copy(out=bias_u[:, nh * N_TILE : (nh + 1) * N_TILE], in_=acc[:])
-
         bias_cand = keep.tile([P, N_TILE], F32)
 
-        def broadcast_candidate_bias():
-            acc = psum.tile([P, N_TILE], F32, tag="bank")
-            nc.tensor.matmul(
-                out=acc[:],
-                lhsT=ones[:],
-                rhs=bias_row[:, CAND * WIDTH : CAND * WIDTH + N_TILE],
-                start=True,
-                stop=True,
-            )
-            nc.scalar.copy(out=bias_cand[:], in_=acc[:])
-
-        bias_r = keep.tile([P, G, PACK], F32)
-        bias_c = keep.tile([P, CT], F32)
-
-        def spread_bias():
-            acc = psum.tile([P, 2, CT], F32, tag="bank")
-            for j in range(CT):
-                first = (j // PACK) * N_TILE + j % PACK
+        def broadcast_bias(first_row):
+            acc = psum.tile([P, PACK, P], F32, tag="bank")
+            for j in range(PACK):
+                row = first_row + j
                 nc.tensor.matmul(
-                    out=acc[:, 0, j : j + 1],
-                    lhsT=bias_row[:, first : first + N_TILE - PACK + 1 : PACK],
-                    rhs=ones[:, 0:1],
+                    out=acc[:, j, :],
+                    lhsT=ident_bf[:, row : row + 1].to_broadcast([P, P]),
+                    rhs=bias_rows[:],
                     start=True,
                     stop=True,
                 )
-            for j in range(CT):
-                first = CAND * WIDTH + j * P
-                nc.tensor.matmul(
-                    out=acc[:, 1, j : j + 1], lhsT=bias_row[:, first : first + P], rhs=ones[:, 0:1], start=True, stop=True
-                )
-            nc.scalar.copy(out=bias_r[:].rearrange("p g t -> p (g t)"), in_=acc[:, 0, :])
-            nc.scalar.copy(out=bias_c[:], in_=acc[:, 1, :])
+            return acc[:].rearrange("p j n -> p (j n)")
+
+        bias_c = keep.tile([P, 2 * CT], F32)
+
+        def spread_candidate_bias():
+            turned = psum.tile([P, P], BF16, tag="bank")
+            nc.tensor.transpose(out=turned[:], in_=bias_rows[:], identity=ident_bf[:])
+            nc.scalar.copy(out=bias_c[:], in_=turned[:, : 2 * CT])
+
+        bias_r = keep.tile([P, G, PACK], F32)
+
+        def spread_reset_bias():
+            acc = psum.tile([P, G, PACK], F32, tag="bank")
+            for g in range(G):
+                for t in range(PACK):
+                    nc.tensor.matmul(
+                        out=acc[:, g, t : t + 1],
+                        lhsT=bias_reset_row[:, g * N_TILE + t : (g + 1) * N_TILE : PACK],
+                        rhs=ident_bf[:, 0:1],
+                        start=True,
+                        stop=True,
+                    )
+            nc.scalar.copy(out=bias_r[:], in_=acc[:])
 
         rh_grouped = keep.tile([P, G, BT, P, PACK], BF16, align_bytes=64)
         rh_codes = keep.tile([P, G, BT, P], U32, align_bytes=64)
@@ -278,7 +276,7 @@ def tile_anothergrucell_kernel(
                 out=cand[:, :count].rearrange("p j b -> p (j b)"),
                 in_=acc[:, : count * P],
                 func=ACT.Tanh,
-                bias=bias_c[:, j : j + 1],
+                bias=bias_c[:, CT + j : CT + j + 1],
             )
             return cand
 
@@ -334,9 +332,11 @@ def tile_anothergrucell_kernel(
         permute_reset_planes(0)
         permute_reset_words(X, 0)
         transpose_inputs(H, 1)
-        spread_bias()
-        broadcast_update_bias()
-        broadcast_candidate_bias()
+        nc.scalar.copy(out=bias_u[:, :N_TILE], in_=broadcast_bias(0))
+        nc.scalar.copy(out=bias_u[:, N_TILE:], in_=broadcast_bias(PACK))
+        nc.scalar.copy(out=bias_cand[:], in_=broadcast_bias(CT))
+        spread_candidate_bias()
+        spread_reset_bias()
         quantise_inputs(H, 1)
         permute_reset_words(H, 0)
         permute_reset_planes(1)

@@ -43,8 +43,7 @@ def tile_anothergrucell_kernel(
         nc.vector.memset(warm[:], 0.0)
         bias_rows = keep.tile([P, P], BF16)
         nc.vector.memset(bias_rows[:].bitcast(I32), 0)
-        bias_reset_row = keep.tile([P, WIDTH], BF16)
-        nc.vector.memset(bias_reset_row[:].bitcast(I32), 0)
+        bias_r = keep.tile([P, G, PACK], BF16)
         reset_planes_in = keep.tile([P, WIDTH], U8, align_bytes=64)
         nc.vector.memset(reset_planes_in[:].bitcast(I32), 0)
         w_planes = keep.tile([P, 2 * WIDTH], U8, align_bytes=64)
@@ -86,15 +85,15 @@ def tile_anothergrucell_kernel(
             )
 
         load_activations(X, 0)
-        nc.sync.dma_start(out=bias_rows[: 2 * CT, :], in_=bias[WIDTH:].rearrange("(j n) -> j n", n=P))
-        nc.sync.dma_start(out=bias_reset_row[0:1, :], in_=bias[:WIDTH].rearrange("(o n) -> o n", o=1))
-        load_activations(H, 0)
-        load_activations(X, 1)
         load_scale_columns(reset_planes_in, X, 0, WIDTH)
-        load_activations(H, 1)
-        load_words(reset_words_in[X][0][:], X, 0, N_TILE)
+        nc.sync.dma_start(out=bias_rows[: 2 * CT, :], in_=bias[WIDTH:].rearrange("(j n) -> j n", n=P))
+        load_activations(H, 0)
+        for s in (X, H):
+            load_activations(s, 1)
         load_scale_columns(reset_planes_in, H, 0, WIDTH)
-        load_words(reset_words_in[H][0][:], H, 0, N_TILE)
+        for w in (X, H):
+            load_words(reset_words_in[w][0][:], w, 0, N_TILE)
+        nc.sync.dma_start(out=bias_r[:], in_=bias[:WIDTH].rearrange("(g p t) -> p g t", g=G, t=PACK))
         for w in (X, H):
             load_words(reset_words_in[w][1][:], w, N_TILE, N_TILE)
         for w in (X, H):
@@ -171,21 +170,6 @@ def tile_anothergrucell_kernel(
             turned = psum.tile([P, P], BF16, tag="bank")
             nc.tensor.transpose(out=turned[:], in_=bias_rows[:], identity=ident_bf[:])
             nc.scalar.copy(out=bias_c[:], in_=turned[:, : 2 * CT])
-
-        bias_r = keep.tile([P, G, PACK], F32)
-
-        def spread_reset_bias():
-            acc = psum.tile([P, G, PACK], F32, tag="bank")
-            for g in range(G):
-                for t in range(PACK):
-                    nc.tensor.matmul(
-                        out=acc[:, g, t : t + 1],
-                        lhsT=bias_reset_row[:, g * N_TILE + t : (g + 1) * N_TILE : PACK],
-                        rhs=ident_bf[:, 0:1],
-                        start=True,
-                        stop=True,
-                    )
-            nc.scalar.copy(out=bias_r[:], in_=acc[:])
 
         rh_grouped = keep.tile([P, G, BT, P, PACK], BF16, align_bytes=64)
         rh_codes = keep.tile([P, G, BT, P], U32, align_bytes=64)
@@ -328,15 +312,14 @@ def tile_anothergrucell_kernel(
         transpose_inputs(H, 0)
         quantise_inputs(H, 0)
         transpose_inputs(X, 1)
-        quantise_inputs(X, 1)
         permute_reset_planes(0)
+        quantise_inputs(X, 1)
         permute_reset_words(X, 0)
         transpose_inputs(H, 1)
         nc.scalar.copy(out=bias_u[:, :N_TILE], in_=broadcast_bias(0))
         nc.scalar.copy(out=bias_u[:, N_TILE:], in_=broadcast_bias(PACK))
         nc.scalar.copy(out=bias_cand[:], in_=broadcast_bias(CT))
         spread_candidate_bias()
-        spread_reset_bias()
         quantise_inputs(H, 1)
         permute_reset_words(H, 0)
         permute_reset_planes(1)

from contextlib import ExitStack

import concourse.mybir as mybir
from concourse.masks import make_identity

F32 = mybir.dt.float32
BF16 = mybir.dt.bfloat16
I32 = mybir.dt.int32
U32 = mybir.dt.uint32
U8 = mybir.dt.uint8
FP8X4 = mybir.dt.float8_e4m3fn_x4
ALU = mybir.AluOpType
ACT = mybir.ActivationFunctionType

P = 128
PACK = 4
K_PASS = P * PACK
BATCH = 512
WIDTH = 1024
BT = BATCH // P
G = WIDTH // K_PASS
KC = 2 * G
N_TILE = 512
NH = WIDTH // N_TILE
CT = WIDTH // P
RESET, UPDATE, CAND = 0, 1, 2
X, H = 0, 1

FLOPS = 2 * BATCH * WIDTH * (3 * WIDTH + 2 * WIDTH + WIDTH)


def tile_anothergrucell_kernel(
    tc, x_t, h_tm1, iw_words, iw_scales, hw_words, hw_scales, bias, out
):
    nc = tc.nc
    with ExitStack() as ctx:
        ctx.enter_context(tc.manual_schedule())
        keep = ctx.enter_context(tc.tile_pool(name="keep", bufs=1))
        work = ctx.enter_context(tc.tile_pool(name="work", bufs=4))
        psum = ctx.enter_context(tc.psum_pool(name="psum", bufs=8))

        warm = keep.tile([P, 1], F32)
        nc.vector.memset(warm[:], 0.0)
        bias_rows = keep.tile([P, P], BF16)
        nc.vector.memset(bias_rows[:].bitcast(I32), 0)
        bias_r = keep.tile([P, G, PACK], BF16)
        reset_planes_in = keep.tile([P, WIDTH], U8, align_bytes=64)
        nc.vector.memset(reset_planes_in[:].bitcast(I32), 0)
        w_planes = keep.tile([P, 2 * WIDTH], U8, align_bytes=64)
        nc.vector.memset(w_planes[:].bitcast(I32), 0)
        ident = keep.tile([P, P], F32)
        make_identity(nc, ident[:])
        ident_bf = keep.tile([P, P], BF16)
        nc.vector.tensor_copy(out=ident_bf[:], in_=ident[:])
        nc.scalar.activation(out=warm[:], in_=warm[:], func=ACT.Sigmoid)

        act_sb = [keep.tile([P, BT, WIDTH], BF16, name="x_sb"), keep.tile([P, BT, WIDTH], BF16, name="h_sb")]
        reset_words_in = [
            [keep.tile([P, G, N_TILE], U32, align_bytes=64, name="reset_words_in_%d%d" % (w, g)) for g in range(G)]
            for w in (X, H)
        ]
        w_words = keep.tile([P, KC, 2 * WIDTH], U32, align_bytes=64)

        def load_activations(s, pair):
            source = (x_t, h_tm1)[s]
            nc.sync.dma_start(
                out=act_sb[s][:, 2 * pair : 2 * pair + 2, :],
                in_=source.rearrange("(p t) k -> p t k", t=BT)[:, 2 * pair : 2 * pair + 2, :],
            )

        def load_scale_columns(planes, w, first, width):
            scales = (iw_scales, hw_scales)[w]
            for q in range(4):
                row = 32 * q + G * PACK * w
                nc.sync.dma_start(
                    out=planes[row : row + G * PACK, :].bitcast(I32),
                    in_=scales[:, PACK * q : PACK * (q + 1), first : first + width].bitcast(I32),
                )

        def load_words(tile_view, w, first, width):
            words = (iw_words, hw_words)[w]
            nc.sync.dma_start(
                out=tile_view.bitcast(I32),
                in_=words.rearrange("g p n t -> p g (n t)")[:, :, PACK * first : PACK * (first + width)].bitcast(I32),
            )

        load_activations(X, 0)
        load_scale_columns(reset_planes_in, X, 0, WIDTH)
        nc.sync.dma_start(out=bias_rows[: 2 * CT, :], in_=bias[WIDTH:].rearrange("(j n) -> j n", n=P))
        load_activations(H, 0)
        for s in (X, H):
            load_activations(s, 1)
        load_scale_columns(reset_planes_in, H, 0, WIDTH)
        for w in (X, H):
            load_words(reset_words_in[w][0][:], w, 0, N_TILE)
        nc.sync.dma_start(out=bias_r[:], in_=bias[:WIDTH].rearrange("(g p t) -> p g t", g=G, t=PACK))
        for w in (X, H):
            load_words(reset_words_in[w][1][:], w, N_TILE, N_TILE)
        for w in (X, H):
            load_scale_columns(w_planes, w, WIDTH, 2 * WIDTH)
        for gate in (UPDATE, CAND):
            for w in (X, H):
                first = (gate - UPDATE) * WIDTH
                load_words(w_words[:, G * w : G * (w + 1), first : first + WIDTH], w, WIDTH + first, WIDTH)

        grouped = keep.tile([P, KC, BT, P, PACK], BF16, align_bytes=64)
        act_codes = keep.tile([P, KC, BT, P], U32, align_bytes=64)
        act_planes = keep.tile([P, KC, BT, P], U8, align_bytes=64)

        def transpose_inputs(s, pair):
            for g in range(G):
                bank = psum.tile([P, 2, 2, P], F32, tag="bank")
                for j in range(2):
                    words = act_sb[s][:, 2 * pair + j, :].bitcast(F32)
                    for half in range(2):
                        nc.tensor.transpose(
                            out=bank[:, j, half, :],
                            in_=words[:, g * K_PASS // 2 + half : (g + 1) * K_PASS // 2 : 2],
                            identity=ident[:],
                        )
                nc.scalar.copy(
                    out=grouped[:, G * s + g, 2 * pair : 2 * pair + 2, :, :].bitcast(F32),
                    in_=bank[:].rearrange("p j half b -> p j b half"),
                )

        def quantise_inputs(s, pair):
            tiles = slice(2 * pair, 2 * pair + 2)
            for kc in range(G * s, G * (s + 1)):
                nc.vector.quantize_mx(
                    out=act_codes[:, kc, tiles, :].rearrange("p j b -> p (j b)").bitcast(FP8X4),
                    scales=act_planes[:, kc, tiles, :].rearrange("p j b -> p (j b)"),
                    in_=grouped[:, kc, tiles, :, :].rearrange("p j b t -> p (j b t)"),
                )

        reset_words = keep.tile([P, KC, G, N_TILE], U32, align_bytes=64)
        reset_planes = keep.tile([P, G, N_TILE], U8, align_bytes=64)

        def permute_reset_planes(g):
            nc.vector.tensor_copy(
                out=reset_planes[:, g, :].rearrange("p (t m) -> p t m", t=PACK),
                in_=reset_planes_in[:, g * N_TILE : (g + 1) * N_TILE].rearrange("p (m t) -> p t m", t=PACK),
            )

        def permute_reset_words(w, g):
            for j in range(G):
                nc.vector.tensor_copy(
                    out=reset_words[:, G * w + j, g, :].bitcast(I32).rearrange("p (t c i) -> p c t i", t=PACK, i=4),
                    in_=reset_words_in[w][g][:, j, :].bitcast(I32).rearrange("p (c i t) -> p c t i", t=PACK, i=4),
                )

        bias_u = keep.tile([P, WIDTH], F32)
        bias_cand = keep.tile([P, N_TILE], F32)

        def broadcast_bias(first_row):
            acc = psum.tile([P, PACK, P], F32, tag="bank")
            for j in range(PACK):
                row = first_row + j
                nc.tensor.matmul(
                    out=acc[:, j, :],
                    lhsT=ident_bf[:, row : row + 1].to_broadcast([P, P]),
                    rhs=bias_rows[:],
                    start=True,
                    stop=True,
                )
            return acc[:].rearrange("p j n -> p (j n)")

        bias_c = keep.tile([P, 2 * CT], F32)

        def spread_candidate_bias():
            turned = psum.tile([P, P], BF16, tag="bank")
            nc.tensor.transpose(out=turned[:], in_=bias_rows[:], identity=ident_bf[:])
            nc.scalar.copy(out=bias_c[:], in_=turned[:, : 2 * CT])

        rh_grouped = keep.tile([P, G, BT, P, PACK], BF16, align_bytes=64)
        rh_codes = keep.tile([P, G, BT, P], U32, align_bytes=64)
        rh_planes = keep.tile([P, G, BT, P], U8, align_bytes=64)
        r_all = keep.tile([P, G, PACK, BATCH], F32)

        def reset_pass(acc, g, t, kc):
            cols = slice(t * P, (t + 1) * P)
            nc.tensor.matmul_mx(
                out=acc[:],
                lhsT=reset_words[:, kc, g, cols].bitcast(FP8X4),
                lhsT_scale=reset_planes[PACK * kc : P, g, cols],
                rhs=act_codes[:, kc].rearrange("p j b -> p (j b)").bitcast(FP8X4),
                rhs_scale=act_planes[:, kc].rearrange("p j b -> p (j b)"),
                start=(kc == 0),
                stop=(kc == KC - 1),
            )

        def reset_sigmoid(acc, g, t):
            nc.scalar.activation(
                out=r_all[:, g, t, :], in_=acc[:], func=ACT.Sigmoid, bias=bias_r[:, g, t : t + 1]
            )

        def reset_times_h(g, bt):
            nc.vector.tensor_tensor(
                out=rh_grouped[:, g, bt],
                in0=r_all[:, g, :, bt * P : (bt + 1) * P].rearrange("p t b -> p b t"),
                in1=grouped[:, G * H + g, bt],
                op=ALU.mult,
            )

        def quantise_rh(g, first_bt, count):
            tiles = slice(first_bt, first_bt + count)
            nc.vector.quantize_mx(
                out=rh_codes[:, g, tiles].rearrange("p j b -> p (j b)").bitcast(FP8X4),
                scales=rh_planes[:, g, tiles].rearrange("p j b -> p (j b)"),
                in_=rh_grouped[:, g, tiles].rearrange("p j b t -> p (j b t)"),
            )

        u_all = keep.tile([P, BT, WIDTH], F32)
        uh_all = keep.tile([P, BT, WIDTH], F32)

        def row_sums(bt, gate, nh):
            first = (gate - UPDATE) * WIDTH + nh * N_TILE
            acc = psum.tile([P, N_TILE], F32, tag="bank")
            for kc in range(KC):
                if gate == CAND and kc >= G:
                    codes, planes = rh_codes[:, kc - G, bt, :], rh_planes[:, kc - G, bt, :]
                else:
                    codes, planes = act_codes[:, kc, bt, :], act_planes[:, kc, bt, :]
                nc.tensor.matmul_mx(
                    out=acc[:],
                    lhsT=codes.bitcast(FP8X4),
                    lhsT_scale=planes,
                    rhs=w_words[:, kc, first : first + N_TILE].bitcast(FP8X4),
                    rhs_scale=w_planes[PACK * kc : P, first : first + N_TILE],
                    start=(kc == 0),
                    stop=(kc == KC - 1),
                )
            return acc

        def update_gate(bt, nh):
            cols = slice(nh * N_TILE, (nh + 1) * N_TILE)
            acc = row_sums(bt, UPDATE, nh)
            nc.vector.tensor_tensor(out=u_all[:, bt, cols], in0=acc[:], in1=bias_u[:, cols], op=ALU.add)
            nc.scalar.activation(out=u_all[:, bt, cols], in_=u_all[:, bt, cols], func=ACT.Sigmoid)
            nc.gpsimd.tensor_tensor(
                out=uh_all[:, bt, cols], in0=u_all[:, bt, cols], in1=act_sb[H][:, bt, cols], op=ALU.mult
            )

        def candidate(j, first_bt, count):
            tiles = slice(first_bt, first_bt + count)
            cols = slice(WIDTH + j * P, WIDTH + (j + 1) * P)
            acc = psum.tile([P, BATCH], F32, tag="bank")
            for kc in range(KC):
                codes, planes = (act_codes[:, kc], act_planes[:, kc]) if kc < G else (rh_codes[:, kc - G], rh_planes[:, kc - G])
                nc.tensor.matmul_mx(
                    out=acc[:, : count * P],
                    lhsT=w_words[:, kc, cols].bitcast(FP8X4),
                    lhsT_scale=w_planes[PACK * kc : P, cols],
                    rhs=codes[:, tiles].rearrange("p j b -> p (j b)").bitcast(FP8X4),
                    rhs_scale=planes[:, tiles].rearrange("p j b -> p (j b)"),
                    start=(kc == 0),
                    stop=(kc == KC - 1),
                )
            cand = work.tile([P, BT, P], F32, tag="cand")
            nc.scalar.activation(
                out=cand[:, :count].rearrange("p j b -> p (j b)"),
                in_=acc[:, : count * P],
                func=ACT.Tanh,
                bias=bias_c[:, CT + j : CT + j + 1],
            )
            return cand

        def candidate_rows(bt):
            acc = row_sums(bt, CAND, 0)
            cand = work.tile([P, N_TILE], F32, tag="cand_rows")
            nc.vector.tensor_tensor(out=cand[:], in0=acc[:], in1=bias_cand[:], op=ALU.add)
            nc.scalar.activation(out=cand[:], in_=cand[:], func=ACT.Tanh)
            return cand

        def transpose_candidate(count, cand):
            bank = psum.tile([P, BT, P], F32, tag="bank")
            for i in range(count):
                nc.tensor.transpose(out=bank[:, i, :], in_=cand[:, i, :], identity=ident[:])
            return bank

        def blend_product(j, first_bt, count, bank):
            if count == 0:
                rest = work.tile([P, N_TILE], F32, tag="rest_rows")
                nc.vector.scalar_tensor_tensor(
                    out=rest[:], in0=u_all[:, j, :N_TILE], scalar=1.0, in1=bank[:], op0=ALU.subtract, op1=ALU.mult
                )
                return rest
            rest = work.tile([P, BT, P], F32, tag="rest")
            nc.vector.scalar_tensor_tensor(
                out=rest[:, :count],
                in0=u_all[:, first_bt : first_bt + count, j * P : (j + 1) * P],
                scalar=1.0,
                in1=bank[:, :count],
                op0=ALU.subtract,
                op1=ALU.mult,
            )
            return rest

        def blend_and_store(j, first_bt, count, rest):
            if count == 0:
                h_new = work.tile([P, N_TILE], F32, tag="h_new_rows")
                nc.vector.tensor_tensor(out=h_new[:], in0=uh_all[:, j, :N_TILE], in1=rest[:], op=ALU.subtract)
                nc.sync.dma_start(out=out.rearrange("(p t) n -> p t n", t=BT)[:, j, :N_TILE], in_=h_new[:])
                return
            tiles = slice(first_bt, first_bt + count)
            cols = slice(j * P, (j + 1) * P)
            h_new = work.tile([P, BT, P], F32, tag="h_new")
            nc.vector.tensor_tensor(out=h_new[:, :count], in0=uh_all[:, tiles, cols], in1=rest[:, :count], op=ALU.subtract)
            nc.sync.dma_start(out=out.rearrange("(p t) n -> p t n", t=BT)[:, tiles, cols], in_=h_new[:, :count])

        transpose_inputs(X, 0)
        quantise_inputs(X, 0)
        transpose_inputs(H, 0)
        quantise_inputs(H, 0)
        transpose_inputs(X, 1)
        permute_reset_planes(0)
        quantise_inputs(X, 1)
        permute_reset_words(X, 0)
        transpose_inputs(H, 1)
        nc.scalar.copy(out=bias_u[:, :N_TILE], in_=broadcast_bias(0))
        nc.scalar.copy(out=bias_u[:, N_TILE:], in_=broadcast_bias(PACK))
        nc.scalar.copy(out=bias_cand[:], in_=broadcast_bias(CT))
        spread_candidate_bias()
        quantise_inputs(H, 1)
        permute_reset_words(H, 0)
        permute_reset_planes(1)
        for w in (X, H):
            permute_reset_words(w, 1)

        sums = []
        for t in range(PACK):
            acc = psum.tile([P, BATCH], F32, tag="bank")
            sums.append(acc)
            for kc in range(G):
                reset_pass(acc, 0, t, kc)
        for t in range(PACK):
            for kc in range(G, KC):
                reset_pass(sums[t], 0, t, kc)
            reset_sigmoid(sums[t], 0, t)
        for t in range(PACK):
            acc = psum.tile([P, BATCH], F32, tag="bank")
            for kc in range(KC):
                reset_pass(acc, 1, t, kc)
            reset_sigmoid(acc, 1, t)
        for bt in range(BT):
            reset_times_h(0, bt)
        quantise_rh(0, 0, BT)
        reset_times_h(1, 0)
        for bt in range(1, BT):
            reset_times_h(1, bt)
            quantise_rh(1, bt - 1, 1)
        update_gate(0, 0)
        quantise_rh(1, BT - 1, 1)
        for bt in range(1, BT):
            update_gate(bt, 0)

        H_ROWS = [("rows", bt) for bt in range(BT)]
        pieces = H_ROWS + [(j, 0, BT) for j in range(PACK, CT - 1)] + [(CT - 1, 0, BT // 2), (CT - 1, BT // 2, BT // 2)]
        cands = []
        rests = []
        for i in range(len(pieces) + 2):
            if i < len(pieces):
                if i < BT:
                    cands.append(candidate_rows(i))
                    update_gate(i, 1)
                else:
                    cands.append(candidate(*pieces[i]))
            if 1 <= i <= len(pieces):
                if i - 1 < BT:
                    rests.append(blend_product(i - 1, 0, 0, cands[i - 1]))
                else:
                    j, first_bt, count = pieces[i - 1]
                    bank = transpose_candidate(count, cands[i - 1])
                    rests.append(blend_product(j, first_bt, count, bank))
            if i >= 2:
                if i - 2 < BT:
                    blend_and_store(i - 2, 0, 0, rests[i - 2])
                else:
                    blend_and_store(*pieces[i - 2], rests[i - 2])
